import numpy as np
import ml_dtypes


def mxq(x, axis, fmt="e4m3"):
    dtype, down = {"e4m3": (ml_dtypes.float8_e4m3fn, 7), "e5m2": (ml_dtypes.float8_e5m2, 14)}[fmt]
    v = np.moveaxis(np.asarray(x, np.float32).astype(ml_dtypes.bfloat16).astype(np.float64), axis, -1)
    blocks = v.reshape(v.shape[:-1] + (-1, 32))
    amax = np.abs(blocks).max(-1, keepdims=True)
    byte = np.maximum(np.where(amax > 0, np.frexp(amax)[1] - 1 + 127, 0) - down, 1)
    scale = np.exp2(byte - 127.0)
    codes = (blocks / scale).astype(np.float32).astype(dtype).astype(np.float64)
    return np.moveaxis((codes * scale).reshape(v.shape), -1, axis)


WIDE = False


def mx_kscale(k):
    if not WIDE:
        return np.ones(k)
    levels = np.array([10, -10, 5, -5, 0])
    a = np.random.permutation(np.resize(levels, k // 512 * 4)).reshape(k // 512, 4)
    idx = np.arange(k)
    return np.exp2(a[idx // 512, idx % 128 // 32])


BF16 = ml_dtypes.bfloat16


def bf(x):
    return np.asarray(x, np.float32).astype(BF16)


def f64(x):
    return np.asarray(x).astype(np.float64)


E2M1 = np.array([0.0, 0.5, 1.0, 1.5, 2.0, 3.0, 4.0, 6.0, -0.0, -0.5, -1.0, -1.5, -2.0, -3.0, -4.0, -6.0])


def pack_weight(w, fmt):
    k, n = w.shape
    w = f64(bf(w)).reshape(k // 32, 32, n)
    amax = np.abs(w).max(1)
    if fmt == "e4m3":
        byte = np.frexp(amax)[1] - 1 + 127 - 7
    else:
        mant, ex = np.frexp(amax / 6.0)
        byte = np.where(mant > 0.5, ex, ex - 1) + 127
    byte = np.clip(np.where(amax > 0, byte, 1), 1, 254)
    scaled = (w * np.exp2(127.0 - byte)[:, None, :]).reshape(k, n).astype(np.float32)
    by_word = np.ascontiguousarray(scaled.reshape(k // 512, 128, 4, n).transpose(0, 1, 3, 2))
    if fmt == "e4m3":
        words = by_word.astype(ml_dtypes.float8_e4m3fn).view(np.uint8)
    else:
        c = by_word.astype(ml_dtypes.float4_e2m1fn).view(np.uint8) & 0xF
        words = c[..., 0::2] | (c[..., 1::2] << 4)
    return np.ascontiguousarray(words), np.ascontiguousarray(byte.astype(np.uint8).reshape(k // 512, 16, n))


def unpack_weight(words, scales, fmt):
    g, p, n, _ = words.shape
    if fmt == "e4m3":
        vals = np.ascontiguousarray(words).view(ml_dtypes.float8_e4m3fn).astype(np.float64)
    else:
        nib = np.empty((g, p, n, 4), np.uint8)
        nib[..., 0::2] = words & 0xF
        nib[..., 1::2] = words >> 4
        vals = E2M1[nib]
    vals = vals * np.repeat(np.exp2(scales.astype(np.float64) - 127.0), 8, axis=1)[..., None]
    return vals.transpose(0, 1, 3, 2).reshape(g * 512, n)


N, MUL, RANK, D0, D1, D2 = 128, 1536, 128, 1, 3, 5
DIMS = (D0, D1, D2)
SD = D0 + D1 + D2
NI = len(DIMS)
SCALING = 2.0


def setup_inputs():
    s = mx_kscale(MUL)
    x = bf(np.random.standard_normal((N, SD * MUL)) * np.tile(s, SD))
    a_lora = bf(np.random.standard_normal((N, SD * RANK)) * 0.5)
    stack = np.random.standard_normal((NI, MUL, MUL)) / s[None, :, None]
    words, scales = pack_weight(stack.reshape(-1, MUL), "e4m3")
    w_lora_b = bf(np.random.standard_normal((NI, RANK, MUL)))
    return {"x": x,
            "a_lora": a_lora,
            "w_base_words": words,
            "w_base_scales": scales,
            "w_lora_b": w_lora_b}


def reference(x, a_lora, w_base_words, w_base_scales, w_lora_b):
    x, a_lora, w_lora_b = f64(x), f64(a_lora), f64(w_lora_b)
    w_base = unpack_weight(w_base_words, w_base_scales, "e4m3").reshape(NI, MUL, MUL)
    pw_base = 1.0 / np.sqrt(MUL)
    pw_b = 1.0 / np.sqrt(RANK)
    n = x.shape[0]
    outs = []
    off = 0
    offa = 0
    for k, d in enumerate(DIMS):
        seg = x[:, off:off + d * MUL].reshape(n * d, MUL)
        y = pw_base * (mxq(seg, 1, "e4m3") @ w_base[k])
        a = a_lora[:, offa:offa + d * RANK].reshape(n * d, RANK)
        b = pw_b * (a @ w_lora_b[k])
        outs.append((y + SCALING * b).reshape(n, d * MUL))
        off += d * MUL
        offa += d * RANK
    return np.concatenate(outs, axis=-1)

@@ -1,0 +1,133 @@
+import math
+
+import concourse.mybir as mybir
+from concourse.masks import make_identity
+
+F32 = mybir.dt.float32
+BF16 = mybir.dt.bfloat16
+I32 = mybir.dt.int32
+U32 = mybir.dt.uint32
+U8 = mybir.dt.uint8
+FP8X4 = mybir.dt.float8_e4m3fn_x4
+MULT = mybir.AluOpType.mult
+ADD = mybir.AluOpType.add
+
+P = 128
+PACK = 4
+K_PASS = P * PACK
+MUL = 1536
+PASSES = MUL // K_PASS
+N_TILE = 512
+N_TILES = MUL // N_TILE
+COMPONENTS = (1, 3, 5)
+FIRST_BLOCK = (0, 1, 4)
+BLOCKS = sum(COMPONENTS)
+WORDS = K_PASS // 2
+
+IRREP_ORDER = (2, 1, 0)
+AHEAD = COMPONENTS[IRREP_ORDER[0]]
+
+BASE_FACTOR = 1.0 / math.sqrt(MUL)
+LORA_FACTOR = 2.0 / math.sqrt(P)
+
+FLOPS = 2 * P * BLOCKS * MUL * (MUL + P)
+
+
+def tile_loracuetlinear_pa_e_kernel(tc, x, a_lora, w_base_words, w_base_scales, w_lora_b, out):
+    nc = tc.nc
+    block_order = [FIRST_BLOCK[e] + b for e in IRREP_ORDER for b in range(COMPONENTS[e])]
+    irrep_of = [e for e in range(len(COMPONENTS)) for b in range(COMPONENTS[e])]
+
+    with tc.tile_pool(name="keep", bufs=1) as keep, tc.psum_pool(name="psum_t", bufs=3) as psum_t, tc.psum_pool(
+        name="psum_lora", bufs=2
+    ) as psum_lora, tc.psum_pool(name="psum_mx", bufs=3) as psum_mx, tc.manual_schedule():
+        a_sb = keep.tile([P, BLOCKS * P], BF16)
+        aT_sb = keep.tile([P, BLOCKS, P], BF16)
+        ident_bf16 = keep.tile([P, P], BF16)
+        ident_f32 = keep.tile([P, P], F32)
+        x_sb = [keep.tile([P, MUL], BF16, name="x_sb%d" % j) for j in range(BLOCKS)]
+        b_sb = [keep.tile([P, MUL], BF16, name="b_sb%d" % e) for e in range(len(COMPONENTS))]
+        w_words = [keep.tile([P, MUL], U32, name="w_words%d" % g, align_bytes=64) for g in range(BLOCKS)]
+        w_scales = [keep.tile([P, MUL], U8, name="w_scales%d" % e, align_bytes=64) for e in range(len(COMPONENTS))]
+        grouped = [keep.tile([P, PASSES, K_PASS], BF16, name="grouped%d" % j, align_bytes=64) for j in range(BLOCKS)]
+        x_codes = [keep.tile([P, PASSES, P], U32, name="x_codes%d" % j, align_bytes=64) for j in range(BLOCKS)]
+        x_scales = [keep.tile([P, PASSES, P], U8, name="x_scales%d" % j, align_bytes=64) for j in range(BLOCKS)]
+        out_sb = [keep.tile([P, MUL], F32, name="out_sb%d" % j) for j in range(BLOCKS)]
+
+        for e in IRREP_ORDER:
+            nc.vector.memset(w_scales[e][:].bitcast(I32), 0)
+        make_identity(nc, ident_bf16[:])
+        make_identity(nc, ident_f32[:])
+
+        nc.sync.dma_start(out=a_sb[:], in_=a_lora)
+        for e in IRREP_ORDER:
+            nc.sync.dma_start(out=b_sb[e][:], in_=w_lora_b[e])
+            for b in range(COMPONENTS[e]):
+                j = FIRST_BLOCK[e] + b
+                nc.sync.dma_start(out=x_sb[j][:], in_=x[:, j * MUL : (j + 1) * MUL])
+            for quadrant in range(4):
+                nc.sync.dma_start(
+                    out=w_scales[e][32 * quadrant : 32 * quadrant + 4 * PASSES, :].bitcast(I32),
+                    in_=w_base_scales[PASSES * e : PASSES * (e + 1), 4 * quadrant : 4 * quadrant + 4, :].bitcast(I32),
+                )
+            for c in range(PASSES):
+                g = PASSES * e + c
+                nc.sync.dma_start(
+                    out=w_words[g][:].bitcast(I32),
+                    in_=w_base_words[g].rearrange("p n t -> p (n t)").bitcast(I32),
+                )
+
+        for e in IRREP_ORDER:
+            first, count = FIRST_BLOCK[e], COMPONENTS[e]
+            aT_ps = psum_t.tile([P, max(COMPONENTS), P], BF16, tag="transposed")
+            for b in range(count):
+                j = first + b
+                nc.tensor.transpose(aT_ps[:, b, :], a_sb[:, j * P : (j + 1) * P], ident_bf16[:])
+            nc.vector.tensor_copy(out=aT_sb[:, first : first + count, :], in_=aT_ps[:, :count, :])
+
+        def prepare_block(j):
+            e = irrep_of[j]
+            x_words = x_sb[j][:].bitcast(F32)
+            for c in range(PASSES):
+                cols = slice(c * N_TILE, (c + 1) * N_TILE)
+                lora_ps = psum_lora.tile([P, N_TILE], F32)
+                nc.tensor.matmul(out=lora_ps[:], lhsT=aT_sb[:, j, :], rhs=b_sb[e][:, cols], start=True, stop=True)
+                xT_ps = psum_t.tile([P, 2, P], F32, tag="transposed")
+                for u in range(2):
+                    nc.tensor.transpose(xT_ps[:, u, :], x_words[:, c * WORDS + u : (c + 1) * WORDS : 2], ident_f32[:])
+                nc.scalar.mul(out=out_sb[j][:, cols], in_=lora_ps[:], mul=LORA_FACTOR)
+                nc.vector.tensor_copy(
+                    out=grouped[j][:, c, :].bitcast(F32).rearrange("p (r u) -> p r u", u=2),
+                    in_=xT_ps[:].rearrange("p u r -> p r u"),
+                )
+            for c in range(PASSES):
+                nc.vector.quantize_mx(
+                    out=x_codes[j][:, c, :].bitcast(FP8X4), scales=x_scales[j][:, c, :], in_=grouped[j][:, c, :]
+                )
+
+        def multiply_block(j):
+            e = irrep_of[j]
+            for i in range(N_TILES):
+                cols = slice(i * N_TILE, (i + 1) * N_TILE)
+                acc = psum_mx.tile([P, N_TILE], F32)
+                for c in range(PASSES):
+                    nc.tensor.matmul_mx(
+                        out=acc[:],
+                        lhsT=x_codes[j][:, c, :].bitcast(FP8X4),
+                        lhsT_scale=x_scales[j][:, c, :],
+                        rhs=w_words[PASSES * e + c][:, cols].bitcast(FP8X4),
+                        rhs_scale=w_scales[e][4 * c : P, cols],
+                        start=(c == 0),
+                        stop=(c == PASSES - 1),
+                    )
+                nc.vector.scalar_tensor_tensor(
+                    out=out_sb[j][:, cols], in0=acc[:], scalar=BASE_FACTOR, in1=out_sb[j][:, cols], op0=MULT, op1=ADD
+                )
+            nc.sync.dma_start(out=out[:, j * MUL : (j + 1) * MUL], in_=out_sb[j][:])
+
+        for j in block_order[:AHEAD]:
+            prepare_block(j)
+        for m in range(BLOCKS):
+            multiply_block(block_order[m])
+            if m + AHEAD < BLOCKS:
+                prepare_block(block_order[m + AHEAD])

@@ -22,7 +22,6 @@ N_TILES = MUL // N_TILE
 COMPONENTS = (1, 3, 5)
 FIRST_BLOCK = (0, 1, 4)
 BLOCKS = sum(COMPONENTS)
-WORDS = K_PASS // 2
 
 IRREP_ORDER = (2, 1, 0)
 AHEAD = COMPONENTS[IRREP_ORDER[0]]
@@ -38,7 +37,9 @@ def tile_loracuetlinear_pa_e_kernel(tc, x, a_lora, w_base_words, w_base_scales, 
     block_order = [FIRST_BLOCK[e] + b for e in IRREP_ORDER for b in range(COMPONENTS[e])]
     irrep_of = [e for e in range(len(COMPONENTS)) for b in range(COMPONENTS[e])]
 
-    with tc.tile_pool(name="keep", bufs=1) as keep, tc.psum_pool(name="psum_t", bufs=3) as psum_t, tc.psum_pool(
+    with tc.tile_pool(name="keep", bufs=1) as keep, tc.tile_pool(name="stage", bufs=3) as stage, tc.psum_pool(
+        name="psum_t", bufs=3
+    ) as psum_t, tc.psum_pool(
         name="psum_lora", bufs=2
     ) as psum_lora, tc.psum_pool(name="psum_mx", bufs=3) as psum_mx, tc.manual_schedule():
         a_sb = keep.tile([P, BLOCKS * P], BF16)
@@ -49,7 +50,6 @@ def tile_loracuetlinear_pa_e_kernel(tc, x, a_lora, w_base_words, w_base_scales, 
         b_sb = [keep.tile([P, MUL], BF16, name="b_sb%d" % e) for e in range(len(COMPONENTS))]
         w_words = [keep.tile([P, MUL], U32, name="w_words%d" % g, align_bytes=64) for g in range(BLOCKS)]
         w_scales = [keep.tile([P, MUL], U8, name="w_scales%d" % e, align_bytes=64) for e in range(len(COMPONENTS))]
-        grouped = [keep.tile([P, PASSES, K_PASS], BF16, name="grouped%d" % j, align_bytes=64) for j in range(BLOCKS)]
         x_codes = [keep.tile([P, PASSES, P], U32, name="x_codes%d" % j, align_bytes=64) for j in range(BLOCKS)]
         x_scales = [keep.tile([P, PASSES, P], U8, name="x_scales%d" % j, align_bytes=64) for j in range(BLOCKS)]
         out_sb = [keep.tile([P, MUL], F32, name="out_sb%d" % j) for j in range(BLOCKS)]
@@ -85,24 +85,32 @@ def tile_loracuetlinear_pa_e_kernel(tc, x, a_lora, w_base_words, w_base_scales, 
                 nc.tensor.transpose(aT_ps[:, b, :], a_sb[:, j * P : (j + 1) * P], ident_bf16[:])
             nc.vector.tensor_copy(out=aT_sb[:, first : first + count, :], in_=aT_ps[:, :count, :])
 
+        x_sorted = {}
+
+        def sort_words(j):
+            x_sorted[j] = stage.tile([P, PASSES, 2, P], F32, name="x_sorted")
+            nc.vector.tensor_copy(
+                out=x_sorted[j][:], in_=x_sb[j][:].bitcast(F32).rearrange("r (c p u) -> r c u p", c=PASSES, u=2)
+            )
+
         def prepare_block(j):
             e = irrep_of[j]
-            x_words = x_sb[j][:].bitcast(F32)
+            grouped = stage.tile([P, PASSES, K_PASS], BF16, align_bytes=64)
             for c in range(PASSES):
                 cols = slice(c * N_TILE, (c + 1) * N_TILE)
                 lora_ps = psum_lora.tile([P, N_TILE], F32)
                 nc.tensor.matmul(out=lora_ps[:], lhsT=aT_sb[:, j, :], rhs=b_sb[e][:, cols], start=True, stop=True)
                 xT_ps = psum_t.tile([P, 2, P], F32, tag="transposed")
                 for u in range(2):
-                    nc.tensor.transpose(xT_ps[:, u, :], x_words[:, c * WORDS + u : (c + 1) * WORDS : 2], ident_f32[:])
+                    nc.tensor.transpose(xT_ps[:, u, :], x_sorted[j][:, c, u, :], ident_f32[:])
                 nc.scalar.mul(out=out_sb[j][:, cols], in_=lora_ps[:], mul=LORA_FACTOR)
                 nc.vector.tensor_copy(
-                    out=grouped[j][:, c, :].bitcast(F32).rearrange("p (r u) -> p r u", u=2),
+                    out=grouped[:, c, :].bitcast(F32).rearrange("p (r u) -> p r u", u=2),
                     in_=xT_ps[:].rearrange("p u r -> p r u"),
                 )
             for c in range(PASSES):
                 nc.vector.quantize_mx(
-                    out=x_codes[j][:, c, :].bitcast(FP8X4), scales=x_scales[j][:, c, :], in_=grouped[j][:, c, :]
+                    out=x_codes[j][:, c, :].bitcast(FP8X4), scales=x_scales[j][:, c, :], in_=grouped[:, c, :]
                 )
 
         def multiply_block(j):
@@ -125,9 +133,14 @@ def tile_loracuetlinear_pa_e_kernel(tc, x, a_lora, w_base_words, w_base_scales, 
                 )
             nc.sync.dma_start(out=out[:, j * MUL : (j + 1) * MUL], in_=out_sb[j][:])
 
-        for j in block_order[:AHEAD]:
-            prepare_block(j)
+        sort_words(block_order[0])
+        for m in range(AHEAD):
+            if m + 1 < AHEAD:
+                sort_words(block_order[m + 1])
+            prepare_block(block_order[m])
         for m in range(BLOCKS):
+            if m + AHEAD < BLOCKS:
+                sort_words(block_order[m + AHEAD])
             multiply_block(block_order[m])
             if m + AHEAD < BLOCKS:
                 prepare_block(block_order[m + AHEAD])

@@ -22,6 +22,7 @@ N_TILES = MUL // N_TILE
 COMPONENTS = (1, 3, 5)
 FIRST_BLOCK = (0, 1, 4)
 BLOCKS = sum(COMPONENTS)
+WORDS = K_PASS // 2
 
 IRREP_ORDER = (2, 1, 0)
 AHEAD = COMPONENTS[IRREP_ORDER[0]]
@@ -37,10 +38,8 @@ def tile_loracuetlinear_pa_e_kernel(tc, x, a_lora, w_base_words, w_base_scales, 
     block_order = [FIRST_BLOCK[e] + b for e in IRREP_ORDER for b in range(COMPONENTS[e])]
     irrep_of = [e for e in range(len(COMPONENTS)) for b in range(COMPONENTS[e])]
 
-    with tc.tile_pool(name="keep", bufs=1) as keep, tc.tile_pool(name="stage", bufs=3) as stage, tc.psum_pool(
-        name="psum_t", bufs=3
-    ) as psum_t, tc.psum_pool(
-        name="psum_lora", bufs=2
+    with tc.tile_pool(name="keep", bufs=1) as keep, tc.psum_pool(name="psum_t", bufs=2) as psum_t, tc.psum_pool(
+        name="psum_lora", bufs=PASSES
     ) as psum_lora, tc.psum_pool(name="psum_mx", bufs=3) as psum_mx, tc.manual_schedule():
         a_sb = keep.tile([P, BLOCKS * P], BF16)
         aT_sb = keep.tile([P, BLOCKS, P], BF16)
@@ -50,6 +49,7 @@ def tile_loracuetlinear_pa_e_kernel(tc, x, a_lora, w_base_words, w_base_scales, 
         b_sb = [keep.tile([P, MUL], BF16, name="b_sb%d" % e) for e in range(len(COMPONENTS))]
         w_words = [keep.tile([P, MUL], U32, name="w_words%d" % g, align_bytes=64) for g in range(BLOCKS)]
         w_scales = [keep.tile([P, MUL], U8, name="w_scales%d" % e, align_bytes=64) for e in range(len(COMPONENTS))]
+        grouped = [keep.tile([P, PASSES, K_PASS], BF16, name="grouped%d" % j, align_bytes=64) for j in range(BLOCKS)]
         x_codes = [keep.tile([P, PASSES, P], U32, name="x_codes%d" % j, align_bytes=64) for j in range(BLOCKS)]
         x_scales = [keep.tile([P, PASSES, P], U8, name="x_scales%d" % j, align_bytes=64) for j in range(BLOCKS)]
         out_sb = [keep.tile([P, MUL], F32, name="out_sb%d" % j) for j in range(BLOCKS)]
@@ -85,32 +85,27 @@ def tile_loracuetlinear_pa_e_kernel(tc, x, a_lora, w_base_words, w_base_scales, 
                 nc.tensor.transpose(aT_ps[:, b, :], a_sb[:, j * P : (j + 1) * P], ident_bf16[:])
             nc.vector.tensor_copy(out=aT_sb[:, first : first + count, :], in_=aT_ps[:, :count, :])
 
-        x_sorted = {}
-
-        def sort_words(j):
-            x_sorted[j] = stage.tile([P, PASSES, 2, P], F32, name="x_sorted")
-            nc.vector.tensor_copy(
-                out=x_sorted[j][:], in_=x_sb[j][:].bitcast(F32).rearrange("r (c p u) -> r c u p", c=PASSES, u=2)
-            )
-
-        def prepare_block(j):
+        def transpose_block(j, vector_copies):
             e = irrep_of[j]
-            grouped = stage.tile([P, PASSES, K_PASS], BF16, align_bytes=64)
+            x_words = x_sb[j][:].bitcast(F32)
             for c in range(PASSES):
                 cols = slice(c * N_TILE, (c + 1) * N_TILE)
-                lora_ps = psum_lora.tile([P, N_TILE], F32)
-                nc.tensor.matmul(out=lora_ps[:], lhsT=aT_sb[:, j, :], rhs=b_sb[e][:, cols], start=True, stop=True)
                 xT_ps = psum_t.tile([P, 2, P], F32, tag="transposed")
                 for u in range(2):
-                    nc.tensor.transpose(xT_ps[:, u, :], x_sorted[j][:, c, u, :], ident_f32[:])
+                    nc.tensor.transpose(xT_ps[:, u, :], x_words[:, c * WORDS + u : (c + 1) * WORDS : 2], ident_f32[:])
+                lora_ps = psum_lora.tile([P, N_TILE], F32)
+                nc.tensor.matmul(out=lora_ps[:], lhsT=aT_sb[:, j, :], rhs=b_sb[e][:, cols], start=True, stop=True)
+                side_by_side = grouped[j][:, c, :].bitcast(F32).rearrange("p (r u) -> p r u", u=2)
+                if vector_copies:
+                    nc.vector.tensor_copy(out=side_by_side, in_=xT_ps[:].rearrange("p u r -> p r u"))
+                else:
+                    nc.scalar.copy(out=side_by_side, in_=xT_ps[:].rearrange("p u r -> p r u"))
                 nc.scalar.mul(out=out_sb[j][:, cols], in_=lora_ps[:], mul=LORA_FACTOR)
-                nc.vector.tensor_copy(
-                    out=grouped[:, c, :].bitcast(F32).rearrange("p (r u) -> p r u", u=2),
-                    in_=xT_ps[:].rearrange("p u r -> p r u"),
-                )
+
+        def quantise_block(j):
             for c in range(PASSES):
                 nc.vector.quantize_mx(
-                    out=x_codes[j][:, c, :].bitcast(FP8X4), scales=x_scales[j][:, c, :], in_=grouped[:, c, :]
+                    out=x_codes[j][:, c, :].bitcast(FP8X4), scales=x_scales[j][:, c, :], in_=grouped[j][:, c, :]
                 )
 
         def multiply_block(j):
@@ -133,14 +128,14 @@ def tile_loracuetlinear_pa_e_kernel(tc, x, a_lora, w_base_words, w_base_scales, 
                 )
             nc.sync.dma_start(out=out[:, j * MUL : (j + 1) * MUL], in_=out_sb[j][:])
 
-        sort_words(block_order[0])
-        for m in range(AHEAD):
-            if m + 1 < AHEAD:
-                sort_words(block_order[m + 1])
-            prepare_block(block_order[m])
+        def prepare_step(s):
+            if s < BLOCKS:
+                transpose_block(block_order[s], vector_copies=(s < AHEAD))
+            if 0 < s <= BLOCKS:
+                quantise_block(block_order[s - 1])
+
+        for s in range(AHEAD):
+            prepare_step(s)
         for m in range(BLOCKS):
-            if m + AHEAD < BLOCKS:
-                sort_words(block_order[m + AHEAD])
             multiply_block(block_order[m])
-            if m + AHEAD < BLOCKS:
-                prepare_block(block_order[m + AHEAD])
+            prepare_step(m + AHEAD)

@@ -21,11 +21,15 @@ N_TILE = 512
 N_TILES = MUL // N_TILE
 COMPONENTS = (1, 3, 5)
 FIRST_BLOCK = (0, 1, 4)
+IRREPS = len(COMPONENTS)
 BLOCKS = sum(COMPONENTS)
 WORDS = K_PASS // 2
+PSUM_BANKS = 8
 
 IRREP_ORDER = (2, 1, 0)
-AHEAD = COMPONENTS[IRREP_ORDER[0]]
+X_LOADS = ((4, 1), (5, 1), (6, 1), (7, 2), (0, 4))
+OUT_STORES = ((4, 3), (7, 2), (1, 1), (2, 1), (3, 1), (0, 1))
+SCALE_TILES = ((5, 4), (1, 4), (0, 1))
 
 BASE_FACTOR = 1.0 / math.sqrt(MUL)
 LORA_FACTOR = 2.0 / math.sqrt(P)
@@ -36,106 +40,163 @@ FLOPS = 2 * P * BLOCKS * MUL * (MUL + P)
 def tile_loracuetlinear_pa_e_kernel(tc, x, a_lora, w_base_words, w_base_scales, w_lora_b, out):
     nc = tc.nc
     block_order = [FIRST_BLOCK[e] + b for e in IRREP_ORDER for b in range(COMPONENTS[e])]
-    irrep_of = [e for e in range(len(COMPONENTS)) for b in range(COMPONENTS[e])]
+    irrep_of = [e for e in range(IRREPS) for b in range(COMPONENTS[e])]
+    first_irrep = IRREP_ORDER[0]
+    all_passes = BLOCKS * PASSES
+    pass_banks = [list(range(q, min(q + 2, all_passes))) for q in range(0, all_passes, 2)]
 
-    with tc.tile_pool(name="keep", bufs=1) as keep, tc.psum_pool(name="psum_t", bufs=2) as psum_t, tc.psum_pool(
-        name="psum_lora", bufs=PASSES
-    ) as psum_lora, tc.psum_pool(name="psum_mx", bufs=3) as psum_mx, tc.manual_schedule():
+    with tc.tile_pool(name="keep", bufs=1) as keep, tc.psum_pool(name="psum", bufs=PSUM_BANKS) as psum, tc.manual_schedule():
         a_sb = keep.tile([P, BLOCKS * P], BF16)
         aT_sb = keep.tile([P, BLOCKS, P], BF16)
         ident_bf16 = keep.tile([P, P], BF16)
         ident_f32 = keep.tile([P, P], F32)
-        x_sb = [keep.tile([P, MUL], BF16, name="x_sb%d" % j) for j in range(BLOCKS)]
-        b_sb = [keep.tile([P, MUL], BF16, name="b_sb%d" % e) for e in range(len(COMPONENTS))]
-        w_words = [keep.tile([P, MUL], U32, name="w_words%d" % g, align_bytes=64) for g in range(BLOCKS)]
-        w_scales = [keep.tile([P, MUL], U8, name="w_scales%d" % e, align_bytes=64) for e in range(len(COMPONENTS))]
-        grouped = [keep.tile([P, PASSES, K_PASS], BF16, name="grouped%d" % j, align_bytes=64) for j in range(BLOCKS)]
-        x_codes = [keep.tile([P, PASSES, P], U32, name="x_codes%d" % j, align_bytes=64) for j in range(BLOCKS)]
-        x_scales = [keep.tile([P, PASSES, P], U8, name="x_scales%d" % j, align_bytes=64) for j in range(BLOCKS)]
-        out_sb = [keep.tile([P, MUL], F32, name="out_sb%d" % j) for j in range(BLOCKS)]
+        x_sb = [keep.tile([P, n * MUL], BF16, name="x_sb%d" % j) for j, n in X_LOADS]
+        b_sb = [keep.tile([P, MUL], BF16, name="b_sb%d" % e) for e in range(IRREPS)]
+        w_first = [keep.tile([P, PASSES, N_TILE], U32, name="w_first%d" % i, align_bytes=64) for i in range(N_TILES)]
+        w_whole = {e: keep.tile([P, PASSES, MUL], U32, name="w_whole%d" % e, align_bytes=64) for e in IRREP_ORDER[1:]}
+        w_scales = [keep.tile([P, MUL], U8, name="w_scales%d" % t, align_bytes=64) for t in range(len(SCALE_TILES))]
+        grouped = [keep.tile([P, len(qs) * K_PASS], BF16, name="grouped%d" % b, align_bytes=64) for b, qs in enumerate(pass_banks)]
+        x_codes = [keep.tile([P, len(qs) * P], U32, name="x_codes%d" % b, align_bytes=64) for b, qs in enumerate(pass_banks)]
+        x_scales = [keep.tile([P, len(qs) * P], U8, name="x_scales%d" % b, align_bytes=64) for b, qs in enumerate(pass_banks)]
+        out_sb = [keep.tile([P, n * MUL], F32, name="out_sb%d" % j) for j, n in OUT_STORES]
 
-        for e in IRREP_ORDER:
-            nc.vector.memset(w_scales[e][:].bitcast(I32), 0)
+        x_words = {}
+        for t, (j0, n) in enumerate(X_LOADS):
+            for b in range(n):
+                x_words[j0 + b] = x_sb[t][:, b * MUL : (b + 1) * MUL].bitcast(F32)
+        out_view = {}
+        for t, (j0, n) in enumerate(OUT_STORES):
+            for b in range(n):
+                out_view[j0 + b] = out_sb[t][:, b * MUL : (b + 1) * MUL]
+        scale_plane = {}
+        for t, (g0, n) in enumerate(SCALE_TILES):
+            for k in range(n):
+                scale_plane[g0 + k] = (t, 4 * k)
+
+        for t in range(len(SCALE_TILES)):
+            nc.vector.memset(w_scales[t][:].bitcast(I32), 0)
         make_identity(nc, ident_bf16[:])
         make_identity(nc, ident_f32[:])
 
-        nc.sync.dma_start(out=a_sb[:], in_=a_lora)
-        for e in IRREP_ORDER:
-            nc.sync.dma_start(out=b_sb[e][:], in_=w_lora_b[e])
-            for b in range(COMPONENTS[e]):
-                j = FIRST_BLOCK[e] + b
-                nc.sync.dma_start(out=x_sb[j][:], in_=x[:, j * MUL : (j + 1) * MUL])
+        def load_x(t):
+            j0, n = X_LOADS[t]
+            nc.sync.dma_start(out=x_sb[t][:], in_=x[:, j0 * MUL : (j0 + n) * MUL])
+
+        def load_scales(t):
+            g0, n = SCALE_TILES[t]
             for quadrant in range(4):
+                rows = slice(4 * quadrant, 4 * quadrant + 4)
+                src = w_base_scales[g0 : g0 + n, rows, :] if n > 1 else w_base_scales[g0, rows, :]
                 nc.sync.dma_start(
-                    out=w_scales[e][32 * quadrant : 32 * quadrant + 4 * PASSES, :].bitcast(I32),
-                    in_=w_base_scales[PASSES * e : PASSES * (e + 1), 4 * quadrant : 4 * quadrant + 4, :].bitcast(I32),
-                )
-            for c in range(PASSES):
-                g = PASSES * e + c
-                nc.sync.dma_start(
-                    out=w_words[g][:].bitcast(I32),
-                    in_=w_base_words[g].rearrange("p n t -> p (n t)").bitcast(I32),
+                    out=w_scales[t][32 * quadrant : 32 * quadrant + 4 * n, :].bitcast(I32), in_=src.bitcast(I32)
                 )
 
-        for e in IRREP_ORDER:
-            first, count = FIRST_BLOCK[e], COMPONENTS[e]
-            aT_ps = psum_t.tile([P, max(COMPONENTS), P], BF16, tag="transposed")
-            for b in range(count):
-                j = first + b
+        nc.sync.dma_start(out=a_sb[:], in_=a_lora)
+        load_x(0)
+        nc.sync.dma_start(out=b_sb[first_irrep][:], in_=w_lora_b[first_irrep])
+        for t in range(1, len(X_LOADS)):
+            load_x(t)
+        load_scales(0)
+        g_first = PASSES * first_irrep
+        for i in range(N_TILES):
+            nc.sync.dma_start(
+                out=w_first[i][:].bitcast(I32),
+                in_=w_base_words[g_first : g_first + PASSES, :, i * N_TILE : (i + 1) * N_TILE, :]
+                .rearrange("g p n t -> p g (n t)")
+                .bitcast(I32),
+            )
+        for t, e in enumerate(IRREP_ORDER[1:]):
+            nc.sync.dma_start(out=b_sb[e][:], in_=w_lora_b[e])
+            load_scales(t + 1)
+            nc.sync.dma_start(
+                out=w_whole[e][:].bitcast(I32),
+                in_=w_base_words[PASSES * e : PASSES * (e + 1)].rearrange("g p n t -> p g (n t)").bitcast(I32),
+            )
+
+        def transpose_a(blocks, on_vector):
+            aT_ps = psum.tile([P, len(blocks), P], BF16, tag="bank", name="aT_ps")
+            for b, j in enumerate(blocks):
                 nc.tensor.transpose(aT_ps[:, b, :], a_sb[:, j * P : (j + 1) * P], ident_bf16[:])
-            nc.vector.tensor_copy(out=aT_sb[:, first : first + count, :], in_=aT_ps[:, :count, :])
+            first = blocks[0]
+            if on_vector:
+                nc.vector.tensor_copy(out=aT_sb[:, first : first + len(blocks), :], in_=aT_ps[:])
+            else:
+                nc.scalar.copy(out=aT_sb[:, first : first + len(blocks), :], in_=aT_ps[:])
 
-        def transpose_block(j, vector_copies):
-            e = irrep_of[j]
-            x_words = x_sb[j][:].bitcast(F32)
-            for c in range(PASSES):
-                cols = slice(c * N_TILE, (c + 1) * N_TILE)
-                xT_ps = psum_t.tile([P, 2, P], F32, tag="transposed")
+        def transpose_bank(b, on_vector):
+            qs = pass_banks[b]
+            xT_ps = psum.tile([P, 2 * len(qs), P], F32, tag="bank", name="xT_ps")
+            for h, q in enumerate(qs):
+                s, c = divmod(q, PASSES)
+                words = x_words[block_order[s]]
                 for u in range(2):
-                    nc.tensor.transpose(xT_ps[:, u, :], x_words[:, c * WORDS + u : (c + 1) * WORDS : 2], ident_f32[:])
-                lora_ps = psum_lora.tile([P, N_TILE], F32)
-                nc.tensor.matmul(out=lora_ps[:], lhsT=aT_sb[:, j, :], rhs=b_sb[e][:, cols], start=True, stop=True)
-                side_by_side = grouped[j][:, c, :].bitcast(F32).rearrange("p (r u) -> p r u", u=2)
-                if vector_copies:
-                    nc.vector.tensor_copy(out=side_by_side, in_=xT_ps[:].rearrange("p u r -> p r u"))
-                else:
-                    nc.scalar.copy(out=side_by_side, in_=xT_ps[:].rearrange("p u r -> p r u"))
-                nc.scalar.mul(out=out_sb[j][:, cols], in_=lora_ps[:], mul=LORA_FACTOR)
+                    nc.tensor.transpose(xT_ps[:, 2 * h + u, :], words[:, c * WORDS + u : (c + 1) * WORDS : 2], ident_f32[:])
+            side_by_side = grouped[b][:].bitcast(F32).rearrange("p (h r u) -> p h r u", h=len(qs), u=2)
+            planes = xT_ps[:].rearrange("p (h u) r -> p h r u", u=2)
+            if on_vector:
+                nc.vector.tensor_copy(out=side_by_side, in_=planes)
+            else:
+                nc.scalar.copy(out=side_by_side, in_=planes)
 
-        def quantise_block(j):
-            for c in range(PASSES):
-                nc.vector.quantize_mx(
-                    out=x_codes[j][:, c, :].bitcast(FP8X4), scales=x_scales[j][:, c, :], in_=grouped[j][:, c, :]
-                )
+        def quantise_bank(b):
+            nc.vector.quantize_mx(out=x_codes[b][:].bitcast(FP8X4), scales=x_scales[b][:], in_=grouped[b][:])
 
-        def multiply_block(j):
+        def lora(j, i):
+            cols = slice(i * N_TILE, (i + 1) * N_TILE)
+            lora_ps = psum.tile([P, N_TILE], F32, tag="bank", name="lora_ps")
+            nc.tensor.matmul(out=lora_ps[:], lhsT=aT_sb[:, j, :], rhs=b_sb[irrep_of[j]][:, cols], start=True, stop=True)
+            nc.scalar.mul(out=out_view[j][:, cols], in_=lora_ps[:], mul=LORA_FACTOR)
+
+        def multiply(s, i):
+            j = block_order[s]
             e = irrep_of[j]
-            for i in range(N_TILES):
-                cols = slice(i * N_TILE, (i + 1) * N_TILE)
-                acc = psum_mx.tile([P, N_TILE], F32)
-                for c in range(PASSES):
-                    nc.tensor.matmul_mx(
-                        out=acc[:],
-                        lhsT=x_codes[j][:, c, :].bitcast(FP8X4),
-                        lhsT_scale=x_scales[j][:, c, :],
-                        rhs=w_words[PASSES * e + c][:, cols].bitcast(FP8X4),
-                        rhs_scale=w_scales[e][4 * c : P, cols],
-                        start=(c == 0),
-                        stop=(c == PASSES - 1),
-                    )
-                nc.vector.scalar_tensor_tensor(
-                    out=out_sb[j][:, cols], in0=acc[:], scalar=BASE_FACTOR, in1=out_sb[j][:, cols], op0=MULT, op1=ADD
+            cols = slice(i * N_TILE, (i + 1) * N_TILE)
+            acc = psum.tile([P, N_TILE], F32, tag="bank", name="acc")
+            for c in range(PASSES):
+                b, h = divmod(PASSES * s + c, 2)
+                t, k = scale_plane[PASSES * e + c]
+                rhs = w_first[i][:, c, :] if e == first_irrep else w_whole[e][:, c, cols]
+                nc.tensor.matmul_mx(
+                    out=acc[:],
+                    lhsT=x_codes[b][:, h * P : (h + 1) * P].bitcast(FP8X4),
+                    lhsT_scale=x_scales[b][:, h * P : (h + 1) * P],
+                    rhs=rhs.bitcast(FP8X4),
+                    rhs_scale=w_scales[t][k:P, cols],
+                    start=(c == 0),
+                    stop=(c == PASSES - 1),
                 )
-            nc.sync.dma_start(out=out[:, j * MUL : (j + 1) * MUL], in_=out_sb[j][:])
+            o = out_view[j][:, cols]
+            nc.vector.scalar_tensor_tensor(out=o, in0=acc[:], scalar=BASE_FACTOR, in1=o, op0=MULT, op1=ADD)
 
-        def prepare_step(s):
-            if s < BLOCKS:
-                transpose_block(block_order[s], vector_copies=(s < AHEAD))
-            if 0 < s <= BLOCKS:
-                quantise_block(block_order[s - 1])
+        first_blocks = [FIRST_BLOCK[first_irrep] + b for b in range(COMPONENTS[first_irrep])]
+        other_blocks = [j for j in range(BLOCKS) if j not in first_blocks]
+        transpose_a(first_blocks, True)
+        done_banks = 0
+        for s in range(len(first_blocks)):
+            ready = [b for b in range(done_banks, len(pass_banks)) if pass_banks[b][-1] < PASSES * (s + 1)]
+            for b in ready:
+                transpose_bank(b, True)
+                if b > 0:
+                    quantise_bank(b - 1)
+            done_banks += len(ready)
+            for i in range(N_TILES):
+                lora(block_order[s], i)
+        transpose_a(other_blocks, False)
+        for b in range(done_banks, len(pass_banks)):
+            transpose_bank(b, (b - done_banks) % 2 == 0)
+            quantise_bank(b - 1)
+        quantise_bank(len(pass_banks) - 1)
 
-        for s in range(AHEAD):
-            prepare_step(s)
-        for m in range(BLOCKS):
-            multiply_block(block_order[m])
-            prepare_step(m + AHEAD)
+        store_after = {j0 + n - 1: t for t, (j0, n) in enumerate(OUT_STORES)}
+        for s in range(BLOCKS):
+            j = block_order[s]
+            for i in range(N_TILES):
+                multiply(s, i)
+                if s + 1 < BLOCKS and block_order[s + 1] in other_blocks:
+                    lora(block_order[s + 1], i)
+                if s == BLOCKS - 1:
+                    cols = slice(i * N_TILE, (i + 1) * N_TILE)
+                    nc.sync.dma_start(out=out[:, j * MUL + i * N_TILE : j * MUL + (i + 1) * N_TILE], in_=out_view[j][:, cols])
+            if s < BLOCKS - 1 and j in store_after:
+                j0, n = OUT_STORES[store_after[j]]
+                nc.sync.dma_start(out=out[:, j0 * MUL : (j0 + n) * MUL], in_=out_sb[store_after[j]][:])

@@ -31,6 +31,12 @@ X_LOADS = ((4, 1), (5, 1), (6, 1), (7, 2), (0, 4))
 OUT_STORES = ((4, 3), (7, 2), (1, 1), (2, 1), (3, 1), (0, 1))
 SCALE_TILES = ((5, 4), (1, 4), (0, 1))
 
+HEAD_LORA = 3
+FIRST_LORA_AHEAD = 3
+LORA_AHEAD = 2
+RUN_BANKS = 2
+FIRST_RUN_AFTER = 1
+
 BASE_FACTOR = 1.0 / math.sqrt(MUL)
 LORA_FACTOR = 2.0 / math.sqrt(P)
 
@@ -43,7 +49,10 @@ def tile_loracuetlinear_pa_e_kernel(tc, x, a_lora, w_base_words, w_base_scales, 
     irrep_of = [e for e in range(IRREPS) for b in range(COMPONENTS[e])]
     first_irrep = IRREP_ORDER[0]
     all_passes = BLOCKS * PASSES
-    pass_banks = [list(range(q, min(q + 2, all_passes))) for q in range(0, all_passes, 2)]
+    first_passes = COMPONENTS[first_irrep] * PASSES
+    pass_banks = [list(range(q, min(q + 2, first_passes))) for q in range(0, first_passes, 2)]
+    pass_banks += [list(range(q, min(q + 2, all_passes))) for q in range(first_passes, all_passes, 2)]
+    bank_of = {q: (b, h) for b, qs in enumerate(pass_banks) for h, q in enumerate(qs)}
 
     with tc.tile_pool(name="keep", bufs=1) as keep, tc.psum_pool(name="psum", bufs=PSUM_BANKS) as psum, tc.manual_schedule():
         a_sb = keep.tile([P, BLOCKS * P], BF16)
@@ -94,7 +103,7 @@ def tile_loracuetlinear_pa_e_kernel(tc, x, a_lora, w_base_words, w_base_scales, 
         nc.sync.dma_start(out=a_sb[:], in_=a_lora)
         load_x(0)
         nc.sync.dma_start(out=b_sb[first_irrep][:], in_=w_lora_b[first_irrep])
-        for t in range(1, len(X_LOADS)):
+        for t in range(1, len(X_LOADS) - 1):
             load_x(t)
         load_scales(0)
         g_first = PASSES * first_irrep
@@ -105,6 +114,7 @@ def tile_loracuetlinear_pa_e_kernel(tc, x, a_lora, w_base_words, w_base_scales, 
                 .rearrange("g p n t -> p g (n t)")
                 .bitcast(I32),
             )
+        load_x(len(X_LOADS) - 1)
         for t, e in enumerate(IRREP_ORDER[1:]):
             nc.sync.dma_start(out=b_sb[e][:], in_=w_lora_b[e])
             load_scales(t + 1)
@@ -153,7 +163,7 @@ def tile_loracuetlinear_pa_e_kernel(tc, x, a_lora, w_base_words, w_base_scales, 
             cols = slice(i * N_TILE, (i + 1) * N_TILE)
             acc = psum.tile([P, N_TILE], F32, tag="bank", name="acc")
             for c in range(PASSES):
-                b, h = divmod(PASSES * s + c, 2)
+                b, h = bank_of[PASSES * s + c]
                 t, k = scale_plane[PASSES * e + c]
                 rhs = w_first[i][:, c, :] if e == first_irrep else w_whole[e][:, c, cols]
                 nc.tensor.matmul_mx(
@@ -170,33 +180,48 @@ def tile_loracuetlinear_pa_e_kernel(tc, x, a_lora, w_base_words, w_base_scales, 
 
         first_blocks = [FIRST_BLOCK[first_irrep] + b for b in range(COMPONENTS[first_irrep])]
         other_blocks = [j for j in range(BLOCKS) if j not in first_blocks]
+        first_banks = [b for b, qs in enumerate(pass_banks) if qs[-1] < first_passes]
+        other_banks = [b for b in range(len(pass_banks)) if b not in first_banks]
         transpose_a(first_blocks, True)
         done_banks = 0
         for s in range(len(first_blocks)):
-            ready = [b for b in range(done_banks, len(pass_banks)) if pass_banks[b][-1] < PASSES * (s + 1)]
+            ready = [b for b in first_banks[done_banks:] if pass_banks[b][-1] < PASSES * (s + 1)]
             for b in ready:
-                transpose_bank(b, True)
+                transpose_bank(b, b % 3 != 2)
                 if b > 0:
                     quantise_bank(b - 1)
             done_banks += len(ready)
-            for i in range(N_TILES):
-                lora(block_order[s], i)
-        transpose_a(other_blocks, False)
-        for b in range(done_banks, len(pass_banks)):
-            transpose_bank(b, (b - done_banks) % 2 == 0)
-            quantise_bank(b - 1)
-        quantise_bank(len(pass_banks) - 1)
+            if s < HEAD_LORA:
+                for i in range(N_TILES):
+                    lora(block_order[s], i)
+        quantise_bank(first_banks[-1])
 
+        woven_lora = {}
+        for s in range(HEAD_LORA, BLOCKS):
+            woven_lora[s - (FIRST_LORA_AHEAD if s < len(first_blocks) else LORA_AHEAD)] = block_order[s]
+        runs = [other_banks[r : r + RUN_BANKS] for r in range(0, len(other_banks), RUN_BANKS)]
+        to_quantise = []
+        quantised = 0
         store_after = {j0 + n - 1: t for t, (j0, n) in enumerate(OUT_STORES)}
         for s in range(BLOCKS):
             j = block_order[s]
             for i in range(N_TILES):
                 multiply(s, i)
-                if s + 1 < BLOCKS and block_order[s + 1] in other_blocks:
-                    lora(block_order[s + 1], i)
+                if quantised < len(to_quantise):
+                    quantise_bank(to_quantise[quantised])
+                    quantised += 1
+                if s in woven_lora:
+                    lora(woven_lora[s], i)
                 if s == BLOCKS - 1:
                     cols = slice(i * N_TILE, (i + 1) * N_TILE)
                     nc.sync.dma_start(out=out[:, j * MUL + i * N_TILE : j * MUL + (i + 1) * N_TILE], in_=out_view[j][:, cols])
             if s < BLOCKS - 1 and j in store_after:
                 j0, n = OUT_STORES[store_after[j]]
                 nc.sync.dma_start(out=out[:, j0 * MUL : (j0 + n) * MUL], in_=out_sb[store_after[j]][:])
+            r = s - FIRST_RUN_AFTER
+            if 0 <= r < len(runs):
+                if r == 0:
+                    transpose_a(other_blocks, False)
+                for b in runs[r]:
+                    transpose_bank(b, False)
+                    to_quantise.append(b)

@@ -31,11 +31,12 @@ X_LOADS = ((4, 1), (5, 1), (6, 1), (7, 2), (0, 4))
 OUT_STORES = ((4, 3), (7, 2), (1, 1), (2, 1), (3, 1), (0, 1))
 SCALE_TILES = ((5, 4), (1, 4), (0, 1))
 
-HEAD_LORA = 3
+HEAD_LORA = (3, 3, 3, 2, 0)
 FIRST_LORA_AHEAD = 3
 LORA_AHEAD = 2
 RUN_BANKS = 2
-FIRST_RUN_AFTER = 1
+FIRST_RUN_AFTER = 2
+WARM_MATMULS = 4
 
 BASE_FACTOR = 1.0 / math.sqrt(MUL)
 LORA_FACTOR = 2.0 / math.sqrt(P)
@@ -60,6 +61,8 @@ def tile_loracuetlinear_pa_e_kernel(tc, x, a_lora, w_base_words, w_base_scales, 
         ident_bf16 = keep.tile([P, P], BF16)
         ident_f32 = keep.tile([P, P], F32)
         x_sb = [keep.tile([P, n * MUL], BF16, name="x_sb%d" % j) for j, n in X_LOADS]
+        x_sorted = keep.tile([P, (BLOCKS - COMPONENTS[first_irrep]) * PASSES * WORDS], F32)
+        warm = keep.tile([P, N_TILE], BF16)
         b_sb = [keep.tile([P, MUL], BF16, name="b_sb%d" % e) for e in range(IRREPS)]
         w_first = [keep.tile([P, PASSES, N_TILE], U32, name="w_first%d" % i, align_bytes=64) for i in range(N_TILES)]
         w_whole = {e: keep.tile([P, PASSES, MUL], U32, name="w_whole%d" % e, align_bytes=64) for e in IRREP_ORDER[1:]}
@@ -77,11 +80,15 @@ def tile_loracuetlinear_pa_e_kernel(tc, x, a_lora, w_base_words, w_base_scales, 
         for t, (j0, n) in enumerate(OUT_STORES):
             for b in range(n):
                 out_view[j0 + b] = out_sb[t][:, b * MUL : (b + 1) * MUL]
+        sorted_words = {}
+        for n, j in enumerate(block_order[COMPONENTS[first_irrep] :]):
+            sorted_words[j] = x_sorted[:, n * PASSES * WORDS : (n + 1) * PASSES * WORDS]
         scale_plane = {}
         for t, (g0, n) in enumerate(SCALE_TILES):
             for k in range(n):
                 scale_plane[g0 + k] = (t, 4 * k)
 
+        nc.vector.memset(warm[:], 0.0)
         for t in range(len(SCALE_TILES)):
             nc.vector.memset(w_scales[t][:].bitcast(I32), 0)
         make_identity(nc, ident_bf16[:])
@@ -138,15 +145,25 @@ def tile_loracuetlinear_pa_e_kernel(tc, x, a_lora, w_base_words, w_base_scales, 
             xT_ps = psum.tile([P, 2 * len(qs), P], F32, tag="bank", name="xT_ps")
             for h, q in enumerate(qs):
                 s, c = divmod(q, PASSES)
-                words = x_words[block_order[s]]
+                j = block_order[s]
                 for u in range(2):
-                    nc.tensor.transpose(xT_ps[:, 2 * h + u, :], words[:, c * WORDS + u : (c + 1) * WORDS : 2], ident_f32[:])
+                    if j in sorted_words:
+                        in_words = sorted_words[j][:, (2 * c + u) * P : (2 * c + u + 1) * P]
+                    else:
+                        in_words = x_words[j][:, c * WORDS + u : (c + 1) * WORDS : 2]
+                    nc.tensor.transpose(xT_ps[:, 2 * h + u, :], in_words, ident_f32[:])
             side_by_side = grouped[b][:].bitcast(F32).rearrange("p (h r u) -> p h r u", h=len(qs), u=2)
             planes = xT_ps[:].rearrange("p (h u) r -> p h r u", u=2)
             if on_vector:
                 nc.vector.tensor_copy(out=side_by_side, in_=planes)
             else:
                 nc.scalar.copy(out=side_by_side, in_=planes)
+
+        def sort_words(j):
+            nc.scalar.copy(
+                out=sorted_words[j].rearrange("p (c u r) -> p c u r", c=PASSES, u=2),
+                in_=x_words[j].rearrange("p (c r u) -> p c u r", c=PASSES, u=2),
+            )
 
         def quantise_bank(b):
             nc.vector.quantize_mx(out=x_codes[b][:].bitcast(FP8X4), scales=x_scales[b][:], in_=grouped[b][:])
@@ -182,8 +199,12 @@ def tile_loracuetlinear_pa_e_kernel(tc, x, a_lora, w_base_words, w_base_scales, 
         other_blocks = [j for j in range(BLOCKS) if j not in first_blocks]
         first_banks = [b for b, qs in enumerate(pass_banks) if qs[-1] < first_passes]
         other_banks = [b for b in range(len(pass_banks)) if b not in first_banks]
+        warm_ps = psum.tile([P, N_TILE], F32, tag="bank", name="warm_ps")
+        for n in range(WARM_MATMULS):
+            nc.tensor.matmul(out=warm_ps[:], lhsT=warm[:, :P], rhs=warm[:], start=True, stop=True)
         transpose_a(first_blocks, True)
         done_banks = 0
+        head_made = 0
         for s in range(len(first_blocks)):
             ready = [b for b in first_banks[done_banks:] if pass_banks[b][-1] < PASSES * (s + 1)]
             for b in ready:
@@ -191,17 +212,19 @@ def tile_loracuetlinear_pa_e_kernel(tc, x, a_lora, w_base_words, w_base_scales, 
                 if b > 0:
                     quantise_bank(b - 1)
             done_banks += len(ready)
-            if s < HEAD_LORA:
-                for i in range(N_TILES):
-                    lora(block_order[s], i)
+            for n in range(HEAD_LORA[s]):
+                lora(block_order[head_made // N_TILES], head_made % N_TILES)
+                head_made += 1
         quantise_bank(first_banks[-1])
 
         woven_lora = {}
-        for s in range(HEAD_LORA, BLOCKS):
-            woven_lora[s - (FIRST_LORA_AHEAD if s < len(first_blocks) else LORA_AHEAD)] = block_order[s]
+        for s in range(head_made // N_TILES, BLOCKS):
+            woven_lora[s - (FIRST_LORA_AHEAD if s < len(first_blocks) else LORA_AHEAD)] = s
         runs = [other_banks[r : r + RUN_BANKS] for r in range(0, len(other_banks), RUN_BANKS)]
         to_quantise = []
         quantised = 0
+        to_sort = block_order[len(first_blocks) :]
+        sorted_blocks = 0
         store_after = {j0 + n - 1: t for t, (j0, n) in enumerate(OUT_STORES)}
         for s in range(BLOCKS):
             j = block_order[s]
@@ -210,8 +233,11 @@ def tile_loracuetlinear_pa_e_kernel(tc, x, a_lora, w_base_words, w_base_scales, 
                 if quantised < len(to_quantise):
                     quantise_bank(to_quantise[quantised])
                     quantised += 1
-                if s in woven_lora:
-                    lora(woven_lora[s], i)
+                if s in woven_lora and N_TILES * woven_lora[s] + i >= head_made:
+                    lora(block_order[woven_lora[s]], i)
+                if s >= FIRST_RUN_AFTER and sorted_blocks < len(to_sort):
+                    sort_words(to_sort[sorted_blocks])
+                    sorted_blocks += 1
                 if s == BLOCKS - 1:
                     cols = slice(i * N_TILE, (i + 1) * N_TILE)
                     nc.sync.dma_start(out=out[:, j * MUL + i * N_TILE : j * MUL + (i + 1) * N_TILE], in_=out_view[j][:, cols])

@@ -32,10 +32,11 @@ OUT_STORES = ((4, 3), (7, 2), (1, 1), (2, 1), (3, 1), (0, 1))
 SCALE_TILES = ((5, 4), (1, 4), (0, 1))
 
 HEAD_LORA = (3, 3, 3, 2, 0)
-FIRST_LORA_AHEAD = 3
-LORA_AHEAD = 2
+LORA_AHEAD = 6
 RUN_BANKS = 2
-FIRST_RUN_AFTER = 2
+SORT_FROM = 6
+FIRST_RUN_AFTER = 8
+RUN_EVERY = 3
 WARM_MATMULS = 4
 
 BASE_FACTOR = 1.0 / math.sqrt(MUL)
@@ -203,6 +204,8 @@ def tile_loracuetlinear_pa_e_kernel(tc, x, a_lora, w_base_words, w_base_scales, 
         for n in range(WARM_MATMULS):
             nc.tensor.matmul(out=warm_ps[:], lhsT=warm[:, :P], rhs=warm[:], start=True, stop=True)
         transpose_a(first_blocks, True)
+        groups = [(s, i) for i in range(N_TILES) for s in range(len(first_blocks))]
+        groups += [(s, i) for s in range(len(first_blocks), BLOCKS) for i in range(N_TILES)]
         done_banks = 0
         head_made = 0
         for s in range(len(first_blocks)):
@@ -213,39 +216,39 @@ def tile_loracuetlinear_pa_e_kernel(tc, x, a_lora, w_base_words, w_base_scales, 
                     quantise_bank(b - 1)
             done_banks += len(ready)
             for n in range(HEAD_LORA[s]):
-                lora(block_order[head_made // N_TILES], head_made % N_TILES)
+                lora(block_order[groups[head_made][0]], groups[head_made][1])
                 head_made += 1
         quantise_bank(first_banks[-1])
 
         woven_lora = {}
-        for s in range(head_made // N_TILES, BLOCKS):
-            woven_lora[s - (FIRST_LORA_AHEAD if s < len(first_blocks) else LORA_AHEAD)] = s
+        for n in range(head_made, len(groups)):
+            woven_lora[n - (head_made if groups[n][0] < len(first_blocks) else LORA_AHEAD)] = n
         runs = [other_banks[r : r + RUN_BANKS] for r in range(0, len(other_banks), RUN_BANKS)]
         to_quantise = []
         quantised = 0
         to_sort = block_order[len(first_blocks) :]
         sorted_blocks = 0
         store_after = {j0 + n - 1: t for t, (j0, n) in enumerate(OUT_STORES)}
-        for s in range(BLOCKS):
+        for g, (s, i) in enumerate(groups):
             j = block_order[s]
-            for i in range(N_TILES):
-                multiply(s, i)
-                if quantised < len(to_quantise):
-                    quantise_bank(to_quantise[quantised])
-                    quantised += 1
-                if s in woven_lora and N_TILES * woven_lora[s] + i >= head_made:
-                    lora(block_order[woven_lora[s]], i)
-                if s >= FIRST_RUN_AFTER and sorted_blocks < len(to_sort):
-                    sort_words(to_sort[sorted_blocks])
-                    sorted_blocks += 1
-                if s == BLOCKS - 1:
-                    cols = slice(i * N_TILE, (i + 1) * N_TILE)
-                    nc.sync.dma_start(out=out[:, j * MUL + i * N_TILE : j * MUL + (i + 1) * N_TILE], in_=out_view[j][:, cols])
-            if s < BLOCKS - 1 and j in store_after:
+            multiply(s, i)
+            if quantised < len(to_quantise):
+                quantise_bank(to_quantise[quantised])
+                quantised += 1
+            if g in woven_lora:
+                s2, i2 = groups[woven_lora[g]]
+                lora(block_order[s2], i2)
+            if g >= SORT_FROM and sorted_blocks < len(to_sort):
+                sort_words(to_sort[sorted_blocks])
+                sorted_blocks += 1
+            if s == BLOCKS - 1:
+                cols = slice(i * N_TILE, (i + 1) * N_TILE)
+                nc.sync.dma_start(out=out[:, j * MUL + i * N_TILE : j * MUL + (i + 1) * N_TILE], in_=out_view[j][:, cols])
+            elif i == N_TILES - 1 and j in store_after:
                 j0, n = OUT_STORES[store_after[j]]
                 nc.sync.dma_start(out=out[:, j0 * MUL : (j0 + n) * MUL], in_=out_sb[store_after[j]][:])
-            r = s - FIRST_RUN_AFTER
-            if 0 <= r < len(runs):
+            r, rest = divmod(g - FIRST_RUN_AFTER, RUN_EVERY)
+            if rest == 0 and 0 <= r < len(runs):
                 if r == 0:
                     transpose_a(other_blocks, False)
                 for b in runs[r]:

@@ -37,6 +37,7 @@ RUN_BANKS = 2
 SORT_FROM = 6
 FIRST_RUN_AFTER = 8
 RUN_EVERY = 3
+LAST_WIDTHS = (256, 128, 128)
 WARM_MATMULS = 4
 
 BASE_FACTOR = 1.0 / math.sqrt(MUL)
@@ -175,15 +176,15 @@ def tile_loracuetlinear_pa_e_kernel(tc, x, a_lora, w_base_words, w_base_scales, 
             nc.tensor.matmul(out=lora_ps[:], lhsT=aT_sb[:, j, :], rhs=b_sb[irrep_of[j]][:, cols], start=True, stop=True)
             nc.scalar.mul(out=out_view[j][:, cols], in_=lora_ps[:], mul=LORA_FACTOR)
 
-        def multiply(s, i):
+        def multiply(s, i, first=0, width=N_TILE):
             j = block_order[s]
             e = irrep_of[j]
-            cols = slice(i * N_TILE, (i + 1) * N_TILE)
-            acc = psum.tile([P, N_TILE], F32, tag="bank", name="acc")
+            cols = slice(i * N_TILE + first, i * N_TILE + first + width)
+            acc = psum.tile([P, width], F32, tag="bank", name="acc")
             for c in range(PASSES):
                 b, h = bank_of[PASSES * s + c]
                 t, k = scale_plane[PASSES * e + c]
-                rhs = w_first[i][:, c, :] if e == first_irrep else w_whole[e][:, c, cols]
+                rhs = w_first[i][:, c, first : first + width] if e == first_irrep else w_whole[e][:, c, cols]
                 nc.tensor.matmul_mx(
                     out=acc[:],
                     lhsT=x_codes[b][:, h * P : (h + 1) * P].bitcast(FP8X4),
@@ -231,7 +232,8 @@ def tile_loracuetlinear_pa_e_kernel(tc, x, a_lora, w_base_words, w_base_scales, 
         store_after = {j0 + n - 1: t for t, (j0, n) in enumerate(OUT_STORES)}
         for g, (s, i) in enumerate(groups):
             j = block_order[s]
-            multiply(s, i)
+            if g < len(groups) - 1:
+                multiply(s, i)
             if quantised < len(to_quantise):
                 quantise_bank(to_quantise[quantised])
                 quantised += 1
@@ -242,8 +244,13 @@ def tile_loracuetlinear_pa_e_kernel(tc, x, a_lora, w_base_words, w_base_scales, 
                 sort_words(to_sort[sorted_blocks])
                 sorted_blocks += 1
             if s == BLOCKS - 1:
-                cols = slice(i * N_TILE, (i + 1) * N_TILE)
-                nc.sync.dma_start(out=out[:, j * MUL + i * N_TILE : j * MUL + (i + 1) * N_TILE], in_=out_view[j][:, cols])
+                first = 0
+                for width in LAST_WIDTHS if g == len(groups) - 1 else (N_TILE,):
+                    if g == len(groups) - 1:
+                        multiply(s, i, first, width)
+                    cols = slice(i * N_TILE + first, i * N_TILE + first + width)
+                    nc.sync.dma_start(out=out[:, j * MUL + cols.start : j * MUL + cols.stop], in_=out_view[j][:, cols])
+                    first += width
             elif i == N_TILES - 1 and j in store_after:
                 j0, n = OUT_STORES[store_after[j]]
                 nc.sync.dma_start(out=out[:, j0 * MUL : (j0 + n) * MUL], in_=out_sb[store_after[j]][:])

@@ -38,6 +38,9 @@ SORT_FROM = 6
 FIRST_RUN_AFTER = 8
 RUN_EVERY = 3
 LAST_WIDTHS = (256, 128, 128)
+W_SCALES_AT = 64
+X_CODES_AT = 128
+X_SCALES_AT = 192
 WARM_MATMULS = 4
 
 BASE_FACTOR = 1.0 / math.sqrt(MUL)
@@ -66,12 +69,15 @@ def tile_loracuetlinear_pa_e_kernel(tc, x, a_lora, w_base_words, w_base_scales, 
         x_sorted = keep.tile([P, (BLOCKS - COMPONENTS[first_irrep]) * PASSES * WORDS], F32)
         warm = keep.tile([P, N_TILE], BF16)
         b_sb = [keep.tile([P, MUL], BF16, name="b_sb%d" % e) for e in range(IRREPS)]
-        w_first = [keep.tile([P, PASSES, N_TILE], U32, name="w_first%d" % i, align_bytes=64) for i in range(N_TILES)]
-        w_whole = {e: keep.tile([P, PASSES, MUL], U32, name="w_whole%d" % e, align_bytes=64) for e in IRREP_ORDER[1:]}
-        w_scales = [keep.tile([P, MUL], U8, name="w_scales%d" % t, align_bytes=64) for t in range(len(SCALE_TILES))]
+        w_first = [keep.tile([P, PASSES, N_TILE], U32, name="w_first%d" % i, align_bytes=256) for i in range(N_TILES)]
+        w_whole = {e: keep.tile([P, PASSES, MUL], U32, name="w_whole%d" % e, align_bytes=256) for e in IRREP_ORDER[1:]}
+        w_scales_tile = [keep.tile([P, W_SCALES_AT + MUL], U8, name="w_scales%d" % t, align_bytes=256) for t in range(len(SCALE_TILES))]
+        w_scales = [tile[:, W_SCALES_AT:] for tile in w_scales_tile]
         grouped = [keep.tile([P, len(qs) * K_PASS], BF16, name="grouped%d" % b, align_bytes=64) for b, qs in enumerate(pass_banks)]
-        x_codes = [keep.tile([P, len(qs) * P], U32, name="x_codes%d" % b, align_bytes=64) for b, qs in enumerate(pass_banks)]
-        x_scales = [keep.tile([P, len(qs) * P], U8, name="x_scales%d" % b, align_bytes=64) for b, qs in enumerate(pass_banks)]
+        x_codes_tile = [keep.tile([P, X_CODES_AT // PACK + len(qs) * P], U32, name="x_codes%d" % b, align_bytes=256) for b, qs in enumerate(pass_banks)]
+        x_codes = [tile[:, X_CODES_AT // PACK :] for tile in x_codes_tile]
+        x_scales_tile = [keep.tile([P, X_SCALES_AT + len(qs) * P], U8, name="x_scales%d" % b, align_bytes=256) for b, qs in enumerate(pass_banks)]
+        x_scales = [tile[:, X_SCALES_AT:] for tile in x_scales_tile]
         out_sb = [keep.tile([P, n * MUL], F32, name="out_sb%d" % j) for j, n in OUT_STORES]
 
         x_words = {}
@@ -92,7 +98,7 @@ def tile_loracuetlinear_pa_e_kernel(tc, x, a_lora, w_base_words, w_base_scales, 
 
         nc.vector.memset(warm[:], 0.0)
         for t in range(len(SCALE_TILES)):
-            nc.vector.memset(w_scales[t][:].bitcast(I32), 0)
+            nc.vector.memset(w_scales_tile[t][:].bitcast(I32), 0)
         make_identity(nc, ident_bf16[:])
         make_identity(nc, ident_f32[:])
 
@@ -168,7 +174,7 @@ def tile_loracuetlinear_pa_e_kernel(tc, x, a_lora, w_base_words, w_base_scales, 
             )
 
         def quantise_bank(b):
-            nc.vector.quantize_mx(out=x_codes[b][:].bitcast(FP8X4), scales=x_scales[b][:], in_=grouped[b][:])
+            nc.vector.quantize_mx(out=x_codes[b].bitcast(FP8X4), scales=x_scales[b], in_=grouped[b][:])
 
         def lora(j, i):
             cols = slice(i * N_TILE, (i + 1) * N_TILE)

@@ -19,6 +19,7 @@ MUL = 1536
 PASSES = MUL // K_PASS
 N_TILE = 512
 N_TILES = MUL // N_TILE
+FIRST_LOADS = ((0, 1), (1, 2))
 COMPONENTS = (1, 3, 5)
 FIRST_BLOCK = (0, 1, 4)
 IRREPS = len(COMPONENTS)
@@ -28,7 +29,7 @@ PSUM_BANKS = 8
 
 IRREP_ORDER = (2, 1, 0)
 X_LOADS = ((4, 1), (5, 1), (6, 1), (7, 2), (0, 4))
-OUT_STORES = ((4, 3), (7, 2), (1, 1), (2, 1), (3, 1), (0, 1))
+OUT_STORES = ((4, 3), (7, 2), (1, 2), (3, 1), (0, 1))
 SCALE_TILES = ((5, 4), (1, 4), (0, 1))
 
 HEAD_LORA = (3, 3, 3, 2, 0)
@@ -69,7 +70,7 @@ def tile_loracuetlinear_pa_e_kernel(tc, x, a_lora, w_base_words, w_base_scales, 
         x_sorted = keep.tile([P, (BLOCKS - COMPONENTS[first_irrep]) * PASSES * WORDS], F32)
         warm = keep.tile([P, N_TILE], BF16)
         b_sb = [keep.tile([P, MUL], BF16, name="b_sb%d" % e) for e in range(IRREPS)]
-        w_first = [keep.tile([P, PASSES, N_TILE], U32, name="w_first%d" % i, align_bytes=256) for i in range(N_TILES)]
+        w_first_tile = [keep.tile([P, PASSES, n * N_TILE], U32, name="w_first%d" % i, align_bytes=256) for i, n in FIRST_LOADS]
         w_whole = {e: keep.tile([P, PASSES, MUL], U32, name="w_whole%d" % e, align_bytes=256) for e in IRREP_ORDER[1:]}
         w_scales_tile = [keep.tile([P, W_SCALES_AT + MUL], U8, name="w_scales%d" % t, align_bytes=256) for t in range(len(SCALE_TILES))]
         w_scales = [tile[:, W_SCALES_AT:] for tile in w_scales_tile]
@@ -91,6 +92,7 @@ def tile_loracuetlinear_pa_e_kernel(tc, x, a_lora, w_base_words, w_base_scales, 
         sorted_words = {}
         for n, j in enumerate(block_order[COMPONENTS[first_irrep] :]):
             sorted_words[j] = x_sorted[:, n * PASSES * WORDS : (n + 1) * PASSES * WORDS]
+        w_first = [w_first_tile[t][:, :, b * N_TILE : (b + 1) * N_TILE] for t, (i, n) in enumerate(FIRST_LOADS) for b in range(n)]
         scale_plane = {}
         for t, (g0, n) in enumerate(SCALE_TILES):
             for k in range(n):
@@ -122,10 +124,10 @@ def tile_loracuetlinear_pa_e_kernel(tc, x, a_lora, w_base_words, w_base_scales, 
             load_x(t)
         load_scales(0)
         g_first = PASSES * first_irrep
-        for i in range(N_TILES):
+        for t, (i, n) in enumerate(FIRST_LOADS):
             nc.sync.dma_start(
-                out=w_first[i][:].bitcast(I32),
-                in_=w_base_words[g_first : g_first + PASSES, :, i * N_TILE : (i + 1) * N_TILE, :]
+                out=w_first_tile[t][:].bitcast(I32),
+                in_=w_base_words[g_first : g_first + PASSES, :, i * N_TILE : (i + n) * N_TILE, :]
                 .rearrange("g p n t -> p g (n t)")
                 .bitcast(I32),
             )
@@ -249,14 +251,15 @@ def tile_loracuetlinear_pa_e_kernel(tc, x, a_lora, w_base_words, w_base_scales, 
             if g >= SORT_FROM and sorted_blocks < len(to_sort):
                 sort_words(to_sort[sorted_blocks])
                 sorted_blocks += 1
-            if s == BLOCKS - 1:
+            if g == len(groups) - 1:
                 first = 0
-                for width in LAST_WIDTHS if g == len(groups) - 1 else (N_TILE,):
-                    if g == len(groups) - 1:
-                        multiply(s, i, first, width)
-                    cols = slice(i * N_TILE + first, i * N_TILE + first + width)
-                    nc.sync.dma_start(out=out[:, j * MUL + cols.start : j * MUL + cols.stop], in_=out_view[j][:, cols])
+                for width in LAST_WIDTHS:
+                    multiply(s, i, first, width)
                     first += width
+            if s == BLOCKS - 1:
+                if i > 0:
+                    cols = slice(0, 2 * N_TILE) if i == 1 else slice(2 * N_TILE, MUL)
+                    nc.sync.dma_start(out=out[:, j * MUL + cols.start : j * MUL + cols.stop], in_=out_view[j][:, cols])
             elif i == N_TILES - 1 and j in store_after:
                 j0, n = OUT_STORES[store_after[j]]
                 nc.sync.dma_start(out=out[:, j0 * MUL : (j0 + n) * MUL], in_=out_sb[store_after[j]][:])

@@ -39,7 +39,7 @@ SORT_FROM = 6
 FIRST_RUN_AFTER = 8
 RUN_EVERY = 3
 LAST_WIDTHS = (256, 128, 128)
-W_SCALES_AT = 64
+W_SCALES_AT = 0
 X_CODES_AT = 128
 X_SCALES_AT = 192
 WARM_MATMULS = 4
@@ -62,14 +62,14 @@ def tile_loracuetlinear_pa_e_kernel(tc, x, a_lora, w_base_words, w_base_scales, 
     bank_of = {q: (b, h) for b, qs in enumerate(pass_banks) for h, q in enumerate(qs)}
 
     with tc.tile_pool(name="keep", bufs=1) as keep, tc.psum_pool(name="psum", bufs=PSUM_BANKS) as psum, tc.manual_schedule():
-        a_sb = keep.tile([P, BLOCKS * P], BF16)
+        a_sb = keep.tile([P, BLOCKS * P], BF16, align_bytes=256)
         aT_sb = keep.tile([P, BLOCKS, P], BF16)
         ident_bf16 = keep.tile([P, P], BF16)
         ident_f32 = keep.tile([P, P], F32)
-        x_sb = [keep.tile([P, n * MUL], BF16, name="x_sb%d" % j) for j, n in X_LOADS]
+        x_sb = [keep.tile([P, n * MUL], BF16, name="x_sb%d" % j, align_bytes=256) for j, n in X_LOADS]
         x_sorted = keep.tile([P, (BLOCKS - COMPONENTS[first_irrep]) * PASSES * WORDS], F32)
         warm = keep.tile([P, N_TILE], BF16)
-        b_sb = [keep.tile([P, MUL], BF16, name="b_sb%d" % e) for e in range(IRREPS)]
+        b_sb = [keep.tile([P, MUL], BF16, name="b_sb%d" % e, align_bytes=256) for e in range(IRREPS)]
         w_first_tile = [keep.tile([P, PASSES, n * N_TILE], U32, name="w_first%d" % i, align_bytes=256) for i, n in FIRST_LOADS]
         w_whole = {e: keep.tile([P, PASSES, MUL], U32, name="w_whole%d" % e, align_bytes=256) for e in IRREP_ORDER[1:]}
         w_scales_tile = [keep.tile([P, W_SCALES_AT + MUL], U8, name="w_scales%d" % t, align_bytes=256) for t in range(len(SCALE_TILES))]
@@ -79,7 +79,7 @@ def tile_loracuetlinear_pa_e_kernel(tc, x, a_lora, w_base_words, w_base_scales, 
         x_codes = [tile[:, X_CODES_AT // PACK :] for tile in x_codes_tile]
         x_scales_tile = [keep.tile([P, X_SCALES_AT + len(qs) * P], U8, name="x_scales%d" % b, align_bytes=256) for b, qs in enumerate(pass_banks)]
         x_scales = [tile[:, X_SCALES_AT:] for tile in x_scales_tile]
-        out_sb = [keep.tile([P, n * MUL], F32, name="out_sb%d" % j) for j, n in OUT_STORES]
+        out_sb = [keep.tile([P, n * MUL], F32, name="out_sb%d" % j, align_bytes=256) for j, n in OUT_STORES]
 
         x_words = {}
         for t, (j0, n) in enumerate(X_LOADS):

@@ -32,12 +32,12 @@ X_LOADS = ((4, 1), (5, 1), (6, 1), (7, 2), (0, 4))
 OUT_STORES = ((4, 3), (7, 2), (1, 2), (3, 1), (0, 1))
 SCALE_TILES = ((5, 4), (1, 4), (0, 1))
 
-HEAD_LORA = (3, 3, 3, 2, 0)
-LORA_AHEAD = 6
-RUN_BANKS = 2
+HEAD_LORA = (3, 3, 2, 2, 1)
+LORA_AHEAD = 7
+RUN_BANKS = 3
 SORT_FROM = 6
 FIRST_RUN_AFTER = 8
-RUN_EVERY = 3
+RUN_EVERY = 4
 LAST_WIDTHS = (256, 128, 128)
 W_SCALES_AT = 0
 X_CODES_AT = 128
@@ -69,7 +69,9 @@ def tile_loracuetlinear_pa_e_kernel(tc, x, a_lora, w_base_words, w_base_scales, 
         x_sb = [keep.tile([P, n * MUL], BF16, name="x_sb%d" % j, align_bytes=256) for j, n in X_LOADS]
         x_sorted = keep.tile([P, (BLOCKS - COMPONENTS[first_irrep]) * PASSES * WORDS], F32)
         warm = keep.tile([P, N_TILE], BF16)
-        b_sb = [keep.tile([P, MUL], BF16, name="b_sb%d" % e, align_bytes=256) for e in range(IRREPS)]
+        b_first = keep.tile([P, MUL], BF16, align_bytes=256)
+        b_others = keep.tile([P, IRREPS - 1, MUL], BF16, align_bytes=256)
+        b_sb = [b_others[:, 0, :], b_others[:, 1, :], b_first[:]]
         w_first_tile = [keep.tile([P, PASSES, n * N_TILE], U32, name="w_first%d" % i, align_bytes=256) for i, n in FIRST_LOADS]
         w_whole = {e: keep.tile([P, PASSES, MUL], U32, name="w_whole%d" % e, align_bytes=256) for e in IRREP_ORDER[1:]}
         w_scales_tile = [keep.tile([P, W_SCALES_AT + MUL], U8, name="w_scales%d" % t, align_bytes=256) for t in range(len(SCALE_TILES))]
@@ -119,7 +121,7 @@ def tile_loracuetlinear_pa_e_kernel(tc, x, a_lora, w_base_words, w_base_scales, 
 
         nc.sync.dma_start(out=a_sb[:], in_=a_lora)
         load_x(0)
-        nc.sync.dma_start(out=b_sb[first_irrep][:], in_=w_lora_b[first_irrep])
+        nc.sync.dma_start(out=b_first[:], in_=w_lora_b[first_irrep])
         for t in range(1, len(X_LOADS) - 1):
             load_x(t)
         load_scales(0)
@@ -133,7 +135,8 @@ def tile_loracuetlinear_pa_e_kernel(tc, x, a_lora, w_base_words, w_base_scales, 
             )
         load_x(len(X_LOADS) - 1)
         for t, e in enumerate(IRREP_ORDER[1:]):
-            nc.sync.dma_start(out=b_sb[e][:], in_=w_lora_b[e])
+            if t == 0:
+                nc.sync.dma_start(out=b_others[:], in_=w_lora_b[0:2].rearrange("e p n -> p e n"))
             load_scales(t + 1)
             nc.sync.dma_start(
                 out=w_whole[e][:].bitcast(I32),
@@ -169,11 +172,13 @@ def tile_loracuetlinear_pa_e_kernel(tc, x, a_lora, w_base_words, w_base_scales, 
             else:
                 nc.scalar.copy(out=side_by_side, in_=planes)
 
-        def sort_words(j):
-            nc.scalar.copy(
-                out=sorted_words[j].rearrange("p (c u r) -> p c u r", c=PASSES, u=2),
-                in_=x_words[j].rearrange("p (c r u) -> p c u r", c=PASSES, u=2),
-            )
+        def sort_words(j, on_gpsimd):
+            side_by_side = sorted_words[j].rearrange("p (c u r) -> p c u r", c=PASSES, u=2)
+            planes = x_words[j].rearrange("p (c r u) -> p c u r", c=PASSES, u=2)
+            if on_gpsimd:
+                nc.gpsimd.tensor_copy(out=side_by_side, in_=planes)
+            else:
+                nc.scalar.copy(out=side_by_side, in_=planes)
 
         def quantise_bank(b):
             nc.vector.quantize_mx(out=x_codes[b].bitcast(FP8X4), scales=x_scales[b], in_=grouped[b][:])
@@ -213,6 +218,7 @@ def tile_loracuetlinear_pa_e_kernel(tc, x, a_lora, w_base_words, w_base_scales, 
         for n in range(WARM_MATMULS):
             nc.tensor.matmul(out=warm_ps[:], lhsT=warm[:, :P], rhs=warm[:], start=True, stop=True)
         transpose_a(first_blocks, True)
+        transpose_a(other_blocks, True)
         groups = [(s, i) for i in range(N_TILES) for s in range(len(first_blocks))]
         groups += [(s, i) for s in range(len(first_blocks), BLOCKS) for i in range(N_TILES)]
         done_banks = 0
@@ -233,6 +239,7 @@ def tile_loracuetlinear_pa_e_kernel(tc, x, a_lora, w_base_words, w_base_scales, 
         for n in range(head_made, len(groups)):
             woven_lora[n - (head_made if groups[n][0] < len(first_blocks) else LORA_AHEAD)] = n
         runs = [other_banks[r : r + RUN_BANKS] for r in range(0, len(other_banks), RUN_BANKS)]
+        run_after = [FIRST_RUN_AFTER + RUN_EVERY * r for r in range(len(runs))]
         to_quantise = []
         quantised = 0
         to_sort = block_order[len(first_blocks) :]
@@ -245,11 +252,12 @@ def tile_loracuetlinear_pa_e_kernel(tc, x, a_lora, w_base_words, w_base_scales, 
             if quantised < len(to_quantise):
                 quantise_bank(to_quantise[quantised])
                 quantised += 1
-            if g in woven_lora:
+            if g in woven_lora and g - 1 not in run_after:
                 s2, i2 = groups[woven_lora[g]]
                 lora(block_order[s2], i2)
-            if g >= SORT_FROM and sorted_blocks < len(to_sort):
-                sort_words(to_sort[sorted_blocks])
+            if g >= SORT_FROM and sorted_blocks < len(to_sort) // 2:
+                for on_gpsimd in (False, True):
+                    sort_words(to_sort[sorted_blocks + 2 * on_gpsimd], on_gpsimd)
                 sorted_blocks += 1
             if g == len(groups) - 1:
                 first = 0
@@ -257,16 +265,16 @@ def tile_loracuetlinear_pa_e_kernel(tc, x, a_lora, w_base_words, w_base_scales, 
                     multiply(s, i, first, width)
                     first += width
             if s == BLOCKS - 1:
-                if i > 0:
-                    cols = slice(0, 2 * N_TILE) if i == 1 else slice(2 * N_TILE, MUL)
+                for first, last in ((), ((0, 1024),), ((1024, 1280), (1280, 1536)))[i]:
+                    cols = slice(first, last)
                     nc.sync.dma_start(out=out[:, j * MUL + cols.start : j * MUL + cols.stop], in_=out_view[j][:, cols])
             elif i == N_TILES - 1 and j in store_after:
                 j0, n = OUT_STORES[store_after[j]]
                 nc.sync.dma_start(out=out[:, j0 * MUL : (j0 + n) * MUL], in_=out_sb[store_after[j]][:])
             r, rest = divmod(g - FIRST_RUN_AFTER, RUN_EVERY)
             if rest == 0 and 0 <= r < len(runs):
-                if r == 0:
-                    transpose_a(other_blocks, False)
                 for b in runs[r]:
                     transpose_bank(b, False)
                     to_quantise.append(b)
+                s2, i2 = groups[woven_lora[g + 1]]
+                lora(block_order[s2], i2)

@@ -29,7 +29,7 @@ PSUM_BANKS = 8
 
 IRREP_ORDER = (2, 1, 0)
 X_LOADS = ((4, 1), (5, 1), (6, 1), (7, 2), (0, 4))
-OUT_STORES = ((4, 3), (7, 2), (1, 2), (3, 1), (0, 1))
+OUT_STORES = ((4, 3), (7, 2), (1, 1), (2, 1), (3, 1), (0, 1))
 SCALE_TILES = ((5, 4), (1, 4), (0, 1))
 
 HEAD_LORA = (3, 3, 2, 2, 1)
@@ -101,8 +101,7 @@ def tile_loracuetlinear_pa_e_kernel(tc, x, a_lora, w_base_words, w_base_scales, 
                 scale_plane[g0 + k] = (t, 4 * k)
 
         nc.vector.memset(warm[:], 0.0)
-        for t in range(len(SCALE_TILES)):
-            nc.vector.memset(w_scales_tile[t][:].bitcast(I32), 0)
+        nc.vector.memset(w_scales_tile[0][:].bitcast(I32), 0)
         make_identity(nc, ident_bf16[:])
         make_identity(nc, ident_f32[:])
 
@@ -110,21 +109,19 @@ def tile_loracuetlinear_pa_e_kernel(tc, x, a_lora, w_base_words, w_base_scales, 
             j0, n = X_LOADS[t]
             nc.sync.dma_start(out=x_sb[t][:], in_=x[:, j0 * MUL : (j0 + n) * MUL])
 
-        def load_scales(t):
+        def load_scales(t, queue, view):
             g0, n = SCALE_TILES[t]
             for quadrant in range(4):
                 rows = slice(4 * quadrant, 4 * quadrant + 4)
                 src = w_base_scales[g0 : g0 + n, rows, :] if n > 1 else w_base_scales[g0, rows, :]
-                nc.sync.dma_start(
-                    out=w_scales[t][32 * quadrant : 32 * quadrant + 4 * n, :].bitcast(I32), in_=src.bitcast(I32)
-                )
+                queue.dma_start(out=w_scales[t][32 * quadrant : 32 * quadrant + 4 * n, :].bitcast(view), in_=src.bitcast(view))
 
         nc.sync.dma_start(out=a_sb[:], in_=a_lora)
         load_x(0)
         nc.sync.dma_start(out=b_first[:], in_=w_lora_b[first_irrep])
         for t in range(1, len(X_LOADS) - 1):
             load_x(t)
-        load_scales(0)
+        load_scales(0, nc.sync, I32)
         g_first = PASSES * first_irrep
         for t, (i, n) in enumerate(FIRST_LOADS):
             nc.sync.dma_start(
@@ -137,7 +134,6 @@ def tile_loracuetlinear_pa_e_kernel(tc, x, a_lora, w_base_words, w_base_scales, 
         for t, e in enumerate(IRREP_ORDER[1:]):
             if t == 0:
                 nc.sync.dma_start(out=b_others[:], in_=w_lora_b[0:2].rearrange("e p n -> p e n"))
-            load_scales(t + 1)
             nc.sync.dma_start(
                 out=w_whole[e][:].bitcast(I32),
                 in_=w_base_words[PASSES * e : PASSES * (e + 1)].rearrange("g p n t -> p g (n t)").bitcast(I32),
@@ -234,6 +230,9 @@ def tile_loracuetlinear_pa_e_kernel(tc, x, a_lora, w_base_words, w_base_scales, 
                 lora(block_order[groups[head_made][0]], groups[head_made][1])
                 head_made += 1
         quantise_bank(first_banks[-1])
+        for t in range(1, len(SCALE_TILES)):
+            nc.vector.memset(w_scales_tile[t][:].bitcast(I32), 0)
+            load_scales(t, nc.gpsimd, F32)
 
         woven_lora = {}
         for n in range(head_made, len(groups)):

import math

import concourse.mybir as mybir
from concourse.masks import make_identity

F32 = mybir.dt.float32
BF16 = mybir.dt.bfloat16
I32 = mybir.dt.int32
U32 = mybir.dt.uint32
U8 = mybir.dt.uint8
FP8X4 = mybir.dt.float8_e4m3fn_x4
MULT = mybir.AluOpType.mult
ADD = mybir.AluOpType.add

P = 128
PACK = 4
K_PASS = P * PACK
MUL = 1536
PASSES = MUL // K_PASS
N_TILE = 512
N_TILES = MUL // N_TILE
FIRST_LOADS = ((0, 1), (1, 2))
COMPONENTS = (1, 3, 5)
FIRST_BLOCK = (0, 1, 4)
IRREPS = len(COMPONENTS)
BLOCKS = sum(COMPONENTS)
WORDS = K_PASS // 2
PSUM_BANKS = 8

IRREP_ORDER = (2, 1, 0)
X_LOADS = ((4, 1), (5, 1), (6, 1), (7, 2), (0, 4))
OUT_STORES = ((4, 3), (7, 2), (1, 1), (2, 1), (3, 1), (0, 1))
SCALE_TILES = ((5, 4), (1, 4), (0, 1))

HEAD_LORA = (3, 3, 2, 2, 1)
LORA_AHEAD = 7
RUN_BANKS = 3
SORT_FROM = 6
FIRST_RUN_AFTER = 8
RUN_EVERY = 4
LAST_WIDTHS = (256, 128, 128)
W_SCALES_AT = 0
X_CODES_AT = 128
X_SCALES_AT = 192
WARM_MATMULS = 4

BASE_FACTOR = 1.0 / math.sqrt(MUL)
LORA_FACTOR = 2.0 / math.sqrt(P)

FLOPS = 2 * P * BLOCKS * MUL * (MUL + P)


def tile_loracuetlinear_pa_e_kernel(tc, x, a_lora, w_base_words, w_base_scales, w_lora_b, out):
    nc = tc.nc
    block_order = [FIRST_BLOCK[e] + b for e in IRREP_ORDER for b in range(COMPONENTS[e])]
    irrep_of = [e for e in range(IRREPS) for b in range(COMPONENTS[e])]
    first_irrep = IRREP_ORDER[0]
    all_passes = BLOCKS * PASSES
    first_passes = COMPONENTS[first_irrep] * PASSES
    pass_banks = [list(range(q, min(q + 2, first_passes))) for q in range(0, first_passes, 2)]
    pass_banks += [list(range(q, min(q + 2, all_passes))) for q in range(first_passes, all_passes, 2)]
    bank_of = {q: (b, h) for b, qs in enumerate(pass_banks) for h, q in enumerate(qs)}

    with tc.tile_pool(name="keep", bufs=1) as keep, tc.psum_pool(name="psum", bufs=PSUM_BANKS) as psum, tc.manual_schedule():
        a_sb = keep.tile([P, BLOCKS * P], BF16, align_bytes=256)
        aT_sb = keep.tile([P, BLOCKS, P], BF16)
        ident_bf16 = keep.tile([P, P], BF16)
        ident_f32 = keep.tile([P, P], F32)
        x_sb = [keep.tile([P, n * MUL], BF16, name="x_sb%d" % j, align_bytes=256) for j, n in X_LOADS]
        x_sorted = keep.tile([P, (BLOCKS - COMPONENTS[first_irrep]) * PASSES * WORDS], F32)
        warm = keep.tile([P, N_TILE], BF16)
        b_first = keep.tile([P, MUL], BF16, align_bytes=256)
        b_others = keep.tile([P, IRREPS - 1, MUL], BF16, align_bytes=256)
        b_sb = [b_others[:, 0, :], b_others[:, 1, :], b_first[:]]
        w_first_tile = [keep.tile([P, PASSES, n * N_TILE], U32, name="w_first%d" % i, align_bytes=256) for i, n in FIRST_LOADS]
        w_whole = {e: keep.tile([P, PASSES, MUL], U32, name="w_whole%d" % e, align_bytes=256) for e in IRREP_ORDER[1:]}
        w_scales_tile = [keep.tile([P, W_SCALES_AT + MUL], U8, name="w_scales%d" % t, align_bytes=256) for t in range(len(SCALE_TILES))]
        w_scales = [tile[:, W_SCALES_AT:] for tile in w_scales_tile]
        grouped = [keep.tile([P, len(qs) * K_PASS], BF16, name="grouped%d" % b, align_bytes=64) for b, qs in enumerate(pass_banks)]
        x_codes_tile = [keep.tile([P, X_CODES_AT // PACK + len(qs) * P], U32, name="x_codes%d" % b, align_bytes=256) for b, qs in enumerate(pass_banks)]
        x_codes = [tile[:, X_CODES_AT // PACK :] for tile in x_codes_tile]
        x_scales_tile = [keep.tile([P, X_SCALES_AT + len(qs) * P], U8, name="x_scales%d" % b, align_bytes=256) for b, qs in enumerate(pass_banks)]
        x_scales = [tile[:, X_SCALES_AT:] for tile in x_scales_tile]
        out_sb = [keep.tile([P, n * MUL], F32, name="out_sb%d" % j, align_bytes=256) for j, n in OUT_STORES]

        x_words = {}
        for t, (j0, n) in enumerate(X_LOADS):
            for b in range(n):
                x_words[j0 + b] = x_sb[t][:, b * MUL : (b + 1) * MUL].bitcast(F32)
        out_view = {}
        for t, (j0, n) in enumerate(OUT_STORES):
            for b in range(n):
                out_view[j0 + b] = out_sb[t][:, b * MUL : (b + 1) * MUL]
        sorted_words = {}
        for n, j in enumerate(block_order[COMPONENTS[first_irrep] :]):
            sorted_words[j] = x_sorted[:, n * PASSES * WORDS : (n + 1) * PASSES * WORDS]
        w_first = [w_first_tile[t][:, :, b * N_TILE : (b + 1) * N_TILE] for t, (i, n) in enumerate(FIRST_LOADS) for b in range(n)]
        scale_plane = {}
        for t, (g0, n) in enumerate(SCALE_TILES):
            for k in range(n):
                scale_plane[g0 + k] = (t, 4 * k)

        nc.vector.memset(warm[:], 0.0)
        nc.vector.memset(w_scales_tile[0][:].bitcast(I32), 0)
        make_identity(nc, ident_bf16[:])
        make_identity(nc, ident_f32[:])

        def load_x(t):
            j0, n = X_LOADS[t]
            nc.sync.dma_start(out=x_sb[t][:], in_=x[:, j0 * MUL : (j0 + n) * MUL])

        def load_scales(t, queue, view):
            g0, n = SCALE_TILES[t]
            for quadrant in range(4):
                rows = slice(4 * quadrant, 4 * quadrant + 4)
                src = w_base_scales[g0 : g0 + n, rows, :] if n > 1 else w_base_scales[g0, rows, :]
                queue.dma_start(out=w_scales[t][32 * quadrant : 32 * quadrant + 4 * n, :].bitcast(view), in_=src.bitcast(view))

        nc.sync.dma_start(out=a_sb[:], in_=a_lora)
        load_x(0)
        nc.sync.dma_start(out=b_first[:], in_=w_lora_b[first_irrep])
        for t in range(1, len(X_LOADS) - 1):
            load_x(t)
        load_scales(0, nc.sync, I32)
        g_first = PASSES * first_irrep
        for t, (i, n) in enumerate(FIRST_LOADS):
            nc.sync.dma_start(
                out=w_first_tile[t][:].bitcast(I32),
                in_=w_base_words[g_first : g_first + PASSES, :, i * N_TILE : (i + n) * N_TILE, :]
                .rearrange("g p n t -> p g (n t)")
                .bitcast(I32),
            )
        load_x(len(X_LOADS) - 1)
        for t, e in enumerate(IRREP_ORDER[1:]):
            if t == 0:
                nc.sync.dma_start(out=b_others[:], in_=w_lora_b[0:2].rearrange("e p n -> p e n"))
            nc.sync.dma_start(
                out=w_whole[e][:].bitcast(I32),
                in_=w_base_words[PASSES * e : PASSES * (e + 1)].rearrange("g p n t -> p g (n t)").bitcast(I32),
            )

        def transpose_a(blocks, on_vector):
            aT_ps = psum.tile([P, len(blocks), P], BF16, tag="bank", name="aT_ps")
            for b, j in enumerate(blocks):
                nc.tensor.transpose(aT_ps[:, b, :], a_sb[:, j * P : (j + 1) * P], ident_bf16[:])
            first = blocks[0]
            if on_vector:
                nc.vector.tensor_copy(out=aT_sb[:, first : first + len(blocks), :], in_=aT_ps[:])
            else:
                nc.scalar.copy(out=aT_sb[:, first : first + len(blocks), :], in_=aT_ps[:])

        def transpose_bank(b, on_vector):
            qs = pass_banks[b]
            xT_ps = psum.tile([P, 2 * len(qs), P], F32, tag="bank", name="xT_ps")
            for h, q in enumerate(qs):
                s, c = divmod(q, PASSES)
                j = block_order[s]
                for u in range(2):
                    if j in sorted_words:
                        in_words = sorted_words[j][:, (2 * c + u) * P : (2 * c + u + 1) * P]
                    else:
                        in_words = x_words[j][:, c * WORDS + u : (c + 1) * WORDS : 2]
                    nc.tensor.transpose(xT_ps[:, 2 * h + u, :], in_words, ident_f32[:])
            side_by_side = grouped[b][:].bitcast(F32).rearrange("p (h r u) -> p h r u", h=len(qs), u=2)
            planes = xT_ps[:].rearrange("p (h u) r -> p h r u", u=2)
            if on_vector:
                nc.vector.tensor_copy(out=side_by_side, in_=planes)
            else:
                nc.scalar.copy(out=side_by_side, in_=planes)

        def sort_words(j, on_gpsimd):
            side_by_side = sorted_words[j].rearrange("p (c u r) -> p c u r", c=PASSES, u=2)
            planes = x_words[j].rearrange("p (c r u) -> p c u r", c=PASSES, u=2)
            if on_gpsimd:
                nc.gpsimd.tensor_copy(out=side_by_side, in_=planes)
            else:
                nc.scalar.copy(out=side_by_side, in_=planes)

        def quantise_bank(b):
            nc.vector.quantize_mx(out=x_codes[b].bitcast(FP8X4), scales=x_scales[b], in_=grouped[b][:])

        def lora(j, i):
            cols = slice(i * N_TILE, (i + 1) * N_TILE)
            lora_ps = psum.tile([P, N_TILE], F32, tag="bank", name="lora_ps")
            nc.tensor.matmul(out=lora_ps[:], lhsT=aT_sb[:, j, :], rhs=b_sb[irrep_of[j]][:, cols], start=True, stop=True)
            nc.scalar.mul(out=out_view[j][:, cols], in_=lora_ps[:], mul=LORA_FACTOR)

        def multiply(s, i, first=0, width=N_TILE):
            j = block_order[s]
            e = irrep_of[j]
            cols = slice(i * N_TILE + first, i * N_TILE + first + width)
            acc = psum.tile([P, width], F32, tag="bank", name="acc")
            for c in range(PASSES):
                b, h = bank_of[PASSES * s + c]
                t, k = scale_plane[PASSES * e + c]
                rhs = w_first[i][:, c, first : first + width] if e == first_irrep else w_whole[e][:, c, cols]
                nc.tensor.matmul_mx(
                    out=acc[:],
                    lhsT=x_codes[b][:, h * P : (h + 1) * P].bitcast(FP8X4),
                    lhsT_scale=x_scales[b][:, h * P : (h + 1) * P],
                    rhs=rhs.bitcast(FP8X4),
                    rhs_scale=w_scales[t][k:P, cols],
                    start=(c == 0),
                    stop=(c == PASSES - 1),
                )
            o = out_view[j][:, cols]
            nc.vector.scalar_tensor_tensor(out=o, in0=acc[:], scalar=BASE_FACTOR, in1=o, op0=MULT, op1=ADD)

        first_blocks = [FIRST_BLOCK[first_irrep] + b for b in range(COMPONENTS[first_irrep])]
        other_blocks = [j for j in range(BLOCKS) if j not in first_blocks]
        first_banks = [b for b, qs in enumerate(pass_banks) if qs[-1] < first_passes]
        other_banks = [b for b in range(len(pass_banks)) if b not in first_banks]
        warm_ps = psum.tile([P, N_TILE], F32, tag="bank", name="warm_ps")
        for n in range(WARM_MATMULS):
            nc.tensor.matmul(out=warm_ps[:], lhsT=warm[:, :P], rhs=warm[:], start=True, stop=True)
        transpose_a(first_blocks, True)
        transpose_a(other_blocks, True)
        groups = [(s, i) for i in range(N_TILES) for s in range(len(first_blocks))]
        groups += [(s, i) for s in range(len(first_blocks), BLOCKS) for i in range(N_TILES)]
        done_banks = 0
        head_made = 0
        for s in range(len(first_blocks)):
            ready = [b for b in first_banks[done_banks:] if pass_banks[b][-1] < PASSES * (s + 1)]
            for b in ready:
                transpose_bank(b, b % 3 != 2)
                if b > 0:
                    quantise_bank(b - 1)
            done_banks += len(ready)
            for n in range(HEAD_LORA[s]):
                lora(block_order[groups[head_made][0]], groups[head_made][1])
                head_made += 1
        quantise_bank(first_banks[-1])
        for t in range(1, len(SCALE_TILES)):
            nc.vector.memset(w_scales_tile[t][:].bitcast(I32), 0)
            load_scales(t, nc.gpsimd, F32)

        woven_lora = {}
        for n in range(head_made, len(groups)):
            woven_lora[n - (head_made if groups[n][0] < len(first_blocks) else LORA_AHEAD)] = n
        runs = [other_banks[r : r + RUN_BANKS] for r in range(0, len(other_banks), RUN_BANKS)]
        run_after = [FIRST_RUN_AFTER + RUN_EVERY * r for r in range(len(runs))]
        to_quantise = []
        quantised = 0
        to_sort = block_order[len(first_blocks) :]
        sorted_blocks = 0
        store_after = {j0 + n - 1: t for t, (j0, n) in enumerate(OUT_STORES)}
        for g, (s, i) in enumerate(groups):
            j = block_order[s]
            if g < len(groups) - 1:
                multiply(s, i)
            if quantised < len(to_quantise):
                quantise_bank(to_quantise[quantised])
                quantised += 1
            if g in woven_lora and g - 1 not in run_after:
                s2, i2 = groups[woven_lora[g]]
                lora(block_order[s2], i2)
            if g >= SORT_FROM and sorted_blocks < len(to_sort) // 2:
                for on_gpsimd in (False, True):
                    sort_words(to_sort[sorted_blocks + 2 * on_gpsimd], on_gpsimd)
                sorted_blocks += 1
            if g == len(groups) - 1:
                first = 0
                for width in LAST_WIDTHS:
                    multiply(s, i, first, width)
                    first += width
            if s == BLOCKS - 1:
                for first, last in ((), ((0, 1024),), ((1024, 1280), (1280, 1536)))[i]:
                    cols = slice(first, last)
                    nc.sync.dma_start(out=out[:, j * MUL + cols.start : j * MUL + cols.stop], in_=out_view[j][:, cols])
            elif i == N_TILES - 1 and j in store_after:
                j0, n = OUT_STORES[store_after[j]]
                nc.sync.dma_start(out=out[:, j0 * MUL : (j0 + n) * MUL], in_=out_sb[store_after[j]][:])
            r, rest = divmod(g - FIRST_RUN_AFTER, RUN_EVERY)
            if rest == 0 and 0 <= r < len(runs):
                for b in runs[r]:
                    transpose_bank(b, False)
                    to_quantise.append(b)
                s2, i2 = groups[woven_lora[g + 1]]
                lora(block_order[s2], i2)
